import numpy as np
import ml_dtypes


def mxq(x, axis, fmt="e4m3"):
    dtype, down = {"e4m3": (ml_dtypes.float8_e4m3fn, 7), "e5m2": (ml_dtypes.float8_e5m2, 14)}[fmt]
    v = np.moveaxis(np.asarray(x, np.float32).astype(ml_dtypes.bfloat16).astype(np.float64), axis, -1)
    blocks = v.reshape(v.shape[:-1] + (-1, 32))
    amax = np.abs(blocks).max(-1, keepdims=True)
    byte = np.maximum(np.where(amax > 0, np.frexp(amax)[1] - 1 + 127, 0) - down, 1)
    scale = np.exp2(byte - 127.0)
    codes = (blocks / scale).astype(np.float32).astype(dtype).astype(np.float64)
    return np.moveaxis((codes * scale).reshape(v.shape), -1, axis)


WIDE = False


def mx_kscale(k):
    if not WIDE:
        return np.ones(k)
    levels = np.array([10, -10, 5, -5, 0])
    if k % 512:
        return np.exp2(np.random.permutation(np.resize(levels, k // 32))).repeat(32)
    a = np.empty((k // 512, 16))
    for p in range(k // 512):
        a[p, :8] = np.random.permutation(np.resize(levels, 8))
        for g in range(8):
            far = levels[np.abs(levels - a[p, g]) >= 10]
            a[p, g + 8] = far[np.random.randint(len(far))]
    return np.exp2(a.ravel()).repeat(32)


BF16 = ml_dtypes.bfloat16


def bf(x):
    return np.asarray(x, np.float32).astype(BF16)


def f64(x):
    return np.asarray(x).astype(np.float64)


B, C, HD, H, W = 2, 512, 128, 32, 32
N = H * W
C2 = 2 * C
C3 = 3 * C


def sigmoid(v):
    return 1.0 / (1.0 + np.exp(-v))


def setup_inputs():
    s = mx_kscale(C3)
    return {
        "z": bf(np.random.standard_normal((B, C2, H, W)) * s[None, :C2, None, None]),
        "h": bf(np.random.standard_normal((B, C, H, W)) * s[None, C2:, None, None]),
        "m": bf(np.random.standard_normal((B, C, H, W))),
        "Wm": bf(np.random.standard_normal((C3, C3)) * 1.5 / np.sqrt(C3) / s[None, :]),
        "bm": bf(np.random.standard_normal(C3) * 0.3),
    }


def reference(z, h, m, Wm, bm):
    x = np.concatenate([f64(z), f64(h)], axis=1).reshape(B, C3, N)
    combined = ((mxq(f64(Wm), 1, "e4m3") @ mxq(x, 1, "e4m3")) + f64(bm)[None, :, None]).reshape(B, C3, H, W)
    mo, mg, mi = combined[:, :C], combined[:, C:C2], combined[:, C2:]
    mi = sigmoid(mi)
    new_m = (1.0 - mi) * f64(m) + mi * np.tanh(mg)
    new_h = sigmoid(mo) * new_m
    return new_h, new_m

@@ -1,0 +1,243 @@
+from contextlib import ExitStack
+
+import concourse.mybir as mybir
+from concourse.masks import make_identity
+
+F32 = mybir.dt.float32
+BF16 = mybir.dt.bfloat16
+U32 = mybir.dt.uint32
+U8 = mybir.dt.uint8
+FP8X4 = mybir.dt.float8_e4m3fn_x4
+ACT = mybir.ActivationFunctionType
+
+P = 128
+PACK = 4
+K_PASS = P * PACK
+BATCH = 2
+C = 512
+C3 = 3 * C
+PIXELS = 1024
+PASSES = C3 // K_PASS
+Z_PASSES = 2
+GATES = 3
+OUT_GATE, CANDIDATE, IN_GATE = 0, 1, 2
+C_TILES = C // P
+N_TILE = 512
+N_TILES = BATCH * PIXELS // N_TILE
+HALVES = PIXELS // N_TILE
+PSUM_BANKS = 8
+W_CHUNKS = GATES * C_TILES * PASSES
+CHUNKS_PER_BANK = 2
+W_BANKS = W_CHUNKS // CHUNKS_PER_BANK
+RUN = 4
+
+FLOPS = 2 * C3 * C3 * BATCH * PIXELS
+
+
+def tile_self_attention_memory_module_pb_kernel(tc, z, h, m, Wm, bm, out_0, out_1):
+    nc = tc.nc
+
+    z_rows = z.rearrange("b c i j -> b c (i j)")
+    h_rows = h.rearrange("b c i j -> b c (i j)")
+    m_tiles = m.rearrange("b (q r) i j -> b q r (i j)", r=C_TILES)
+    new_h_tiles = out_0.rearrange("b (q r) i j -> b q r (i j)", r=C_TILES)
+    new_m_tiles = out_1.rearrange("b (q r) i j -> b q r (i j)", r=C_TILES)
+    w_tiles = Wm.rearrange("(a q r) k -> a q r k", a=GATES, r=C_TILES)
+
+    def pass_rows(b, g):
+        if g < Z_PASSES:
+            return z_rows[b, g * K_PASS : (g + 1) * K_PASS, :]
+        return h_rows[b]
+
+    def pixels_of(n):
+        b, half = divmod(n, HALVES)
+        return b, slice(half * N_TILE, (half + 1) * N_TILE)
+
+    with ExitStack() as ctx:
+        consts = ctx.enter_context(tc.tile_pool(name="consts", bufs=1))
+        resident = ctx.enter_context(tc.tile_pool(name="resident", bufs=1))
+        stage = ctx.enter_context(tc.tile_pool(name="stage", bufs=3))
+        gates = ctx.enter_context(tc.tile_pool(name="gates", bufs=6))
+        psum = ctx.enter_context(tc.psum_pool(name="psum", bufs=PSUM_BANKS))
+
+        w_raw = resident.tile([P, GATES, C_TILES, C3], BF16)
+        x_raw = [
+            resident.tile([P, PASSES, PACK, N_TILE], BF16, name="x_raw%d" % n)
+            for n in range(N_TILES)
+        ]
+        m_sb = [
+            resident.tile([P, C_TILES, N_TILE], BF16, name="m_sb%d" % n) for n in range(N_TILES)
+        ]
+        w_codes = resident.tile([P, W_CHUNKS * P], U32, align_bytes=64)
+        w_scales = resident.tile([P, W_CHUNKS * P], U8, align_bytes=64)
+        x_codes = [
+            resident.tile([P, PASSES * N_TILE], U32, name="x_codes%d" % n, align_bytes=64)
+            for n in range(N_TILES)
+        ]
+        x_scales = [
+            resident.tile([P, PASSES * N_TILE], U8, name="x_scales%d" % n, align_bytes=64)
+            for n in range(N_TILES)
+        ]
+
+        def load_w(a, first_tile):
+            tiles = slice(first_tile, first_tile + 2)
+            nc.sync.dma_start(out=w_raw[:, a, tiles, :], in_=w_tiles[a][:, tiles, :])
+
+        def load_x(n):
+            b, cols = pixels_of(n)
+            for g in range(PASSES):
+                nc.sync.dma_start(
+                    out=x_raw[n][:, g, :, :],
+                    in_=pass_rows(b, g)[:, cols].rearrange("(p t) w -> p t w", t=PACK),
+                )
+
+        def load_m(n):
+            b, cols = pixels_of(n)
+            nc.sync.dma_start(out=m_sb[n][:], in_=m_tiles[b][:, :, cols])
+
+        bias_in = consts.tile([P, GATES, C_TILES], BF16)
+        nc.scalar.dma_start(out=bias_in[:], in_=bm.rearrange("(a q r) -> q a r", a=GATES, r=C_TILES))
+        for a in range(GATES):
+            for first_tile in range(0, C_TILES, 2):
+                load_w(a, first_tile)
+        for n in range(N_TILES):
+            load_x(n)
+            load_m(n)
+
+        warm = consts.tile([P, 1], F32)
+        nc.vector.memset(warm[:], 0.0)
+        warm_out = consts.tile([P, 1], F32)
+        nc.scalar.activation(out=warm_out[:], in_=warm[:], func=ACT.Sigmoid)
+
+        ident = consts.tile([P, P], F32)
+        make_identity(nc, ident[:])
+
+        bias = consts.tile([P, GATES, C_TILES], F32)
+        nc.vector.tensor_copy(out=bias[:], in_=bias_in[:])
+
+        def chunk_of(a, r, g):
+            return (a * C_TILES + r) * PASSES + g
+
+        def turn_w_bank(j):
+            w_turned = psum.tile([P, CHUNKS_PER_BANK, 2, P], F32, tag="bank")
+            for s in range(CHUNKS_PER_BANK):
+                row_tile, g = divmod(j * CHUNKS_PER_BANK + s, PASSES)
+                a, r = divmod(row_tile, C_TILES)
+                words = w_raw[:, a, r, :].bitcast(F32)
+                for u in range(2):
+                    every_second = slice(g * 2 * P + u, (g + 1) * 2 * P, 2)
+                    nc.tensor.transpose(w_turned[:, s, u, :], words[:, every_second], ident[:])
+            w_grouped = stage.tile([P, CHUNKS_PER_BANK * P * PACK], BF16, align_bytes=64)
+            nc.scalar.copy(
+                out=w_grouped[:].bitcast(F32).rearrange("p (s o u) -> p s o u", s=CHUNKS_PER_BANK, u=2),
+                in_=w_turned[:].rearrange("p s u o -> p s o u"),
+            )
+            return w_grouped
+
+        def quantise_w(j, w_grouped):
+            cols = slice(j * CHUNKS_PER_BANK * P, (j + 1) * CHUNKS_PER_BANK * P)
+            nc.vector.quantize_mx(
+                out=w_codes[:, cols].bitcast(FP8X4), scales=w_scales[:, cols], in_=w_grouped[:]
+            )
+
+        def regroup_x(n, g):
+            copy = nc.vector.tensor_copy if n < HALVES else nc.scalar.copy
+            x_grouped = stage.tile([P, N_TILE, PACK], BF16, align_bytes=64)
+            copy(
+                out=x_grouped[:].rearrange("p (c i) t -> p c t i", i=RUN),
+                in_=x_raw[n][:, g, :, :].rearrange("p t (c i) -> p c t i", i=RUN),
+            )
+            return x_grouped
+
+        def quantise_x(n, g, x_grouped):
+            cols = slice(g * N_TILE, (g + 1) * N_TILE)
+            nc.vector.quantize_mx(
+                out=x_codes[n][:, cols].bitcast(FP8X4),
+                scales=x_scales[n][:, cols],
+                in_=x_grouped[:].rearrange("p w t -> p (w t)"),
+            )
+
+        def multiply(n, r, a):
+            acc = psum.tile([P, N_TILE], F32, tag="bank")
+            for g in range(PASSES):
+                w_cols = slice(chunk_of(a, r, g) * P, (chunk_of(a, r, g) + 1) * P)
+                x_cols = slice(g * N_TILE, (g + 1) * N_TILE)
+                nc.tensor.matmul_mx(
+                    out=acc[:],
+                    lhsT=w_codes[:, w_cols].bitcast(FP8X4),
+                    lhsT_scale=w_scales[:, w_cols],
+                    rhs=x_codes[n][:, x_cols].bitcast(FP8X4),
+                    rhs_scale=x_scales[n][:, x_cols],
+                    start=(g == 0),
+                    stop=(g == PASSES - 1),
+                )
+            return acc
+
+        def squash(acc, func, r, a, name):
+            result = gates.tile([P, N_TILE], F32, name=name)
+            nc.scalar.activation(out=result[:], in_=acc[:], func=func, bias=bias[:, a, r : r + 1], scale=1.0)
+            return result
+
+        def gates_of(n, r):
+            acc_g = multiply(n, r, CANDIDATE)
+            acc_i = multiply(n, r, IN_GATE)
+            acc_o = multiply(n, r, OUT_GATE)
+            return {
+                "n": n,
+                "r": r,
+                "cand": squash(acc_g, ACT.Tanh, r, CANDIDATE, "cand"),
+                "gate_i": squash(acc_i, ACT.Sigmoid, r, IN_GATE, "gate_i"),
+                "gate_o": squash(acc_o, ACT.Sigmoid, r, OUT_GATE, "gate_o"),
+            }
+
+        def difference(unit):
+            nc.vector.tensor_sub(out=unit["cand"][:], in0=unit["cand"][:], in1=m_sb[unit["n"]][:, unit["r"], :])
+
+        def gated_step(unit):
+            nc.vector.tensor_mul(out=unit["cand"][:], in0=unit["gate_i"][:], in1=unit["cand"][:])
+
+        def store(tiles, unit, result):
+            b, cols = pixels_of(unit["n"])
+            nc.sync.dma_start(out=tiles[b][:, unit["r"], cols], in_=result[:])
+
+        def new_memory(unit):
+            new_m = gates.tile([P, N_TILE], F32, name="new_m")
+            nc.vector.tensor_add(out=new_m[:], in0=unit["cand"][:], in1=m_sb[unit["n"]][:, unit["r"], :])
+            store(new_m_tiles, unit, new_m)
+            return new_m
+
+        def new_hidden(unit, new_m):
+            nc.vector.tensor_mul(out=unit["gate_o"][:], in0=unit["gate_o"][:], in1=new_m[:])
+            store(new_h_tiles, unit, unit["gate_o"])
+
+        copied = None
+        for j in range(W_BANKS):
+            w_grouped = turn_w_bank(j)
+            if copied is not None:
+                quantise_w(*copied)
+            copied = (j, w_grouped)
+        quantise_w(*copied)
+        copied = None
+        for g in range(PASSES):
+            x_grouped = regroup_x(0, g)
+            if copied is not None:
+                quantise_x(*copied)
+            copied = (0, g, x_grouped)
+
+        earlier = None
+        for n in range(N_TILES):
+            for r in range(C_TILES):
+                if copied is not None:
+                    quantise_x(*copied)
+                    copied = None
+                unit = gates_of(n, r)
+                if n + 1 < N_TILES and r < PASSES:
+                    copied = (n + 1, r, regroup_x(n + 1, r))
+                difference(unit)
+                if earlier is not None:
+                    new_m = new_memory(earlier)
+                gated_step(unit)
+                if earlier is not None:
+                    new_hidden(earlier, new_m)
+                earlier = unit
+        new_hidden(earlier, new_memory(earlier))

@@ -21,14 +21,15 @@ PASSES = C3 // K_PASS
 Z_PASSES = 2
 GATES = 3
 OUT_GATE, CANDIDATE, IN_GATE = 0, 1, 2
+GATE_ORDER = (CANDIDATE, IN_GATE, OUT_GATE)
 C_TILES = C // P
-N_TILE = 512
-N_TILES = BATCH * PIXELS // N_TILE
-HALVES = PIXELS // N_TILE
+HALF = 512
+HALVES = PIXELS // HALF
+BLOCK = 2 * HALF
 PSUM_BANKS = 8
-W_CHUNKS = GATES * C_TILES * PASSES
+ROW_CHUNKS = GATES * PASSES
 CHUNKS_PER_BANK = 2
-W_BANKS = W_CHUNKS // CHUNKS_PER_BANK
+W_GROUP = 4
 RUN = 4
 
 FLOPS = 2 * C3 * C3 * BATCH * PIXELS
@@ -49,60 +50,75 @@ def tile_self_attention_memory_module_pb_kernel(tc, z, h, m, Wm, bm, out_0, out_
             return z_rows[b, g * K_PASS : (g + 1) * K_PASS, :]
         return h_rows[b]
 
-    def pixels_of(n):
-        b, half = divmod(n, HALVES)
-        return b, slice(half * N_TILE, (half + 1) * N_TILE)
+    def pixels(first_half, halves=1):
+        return slice(first_half * HALF, (first_half + halves) * HALF)
 
     with ExitStack() as ctx:
         consts = ctx.enter_context(tc.tile_pool(name="consts", bufs=1))
         resident = ctx.enter_context(tc.tile_pool(name="resident", bufs=1))
-        stage = ctx.enter_context(tc.tile_pool(name="stage", bufs=3))
-        gates = ctx.enter_context(tc.tile_pool(name="gates", bufs=6))
+        stage = ctx.enter_context(tc.tile_pool(name="stage", bufs=4))
+        gates = ctx.enter_context(tc.tile_pool(name="gates", bufs=3))
         psum = ctx.enter_context(tc.psum_pool(name="psum", bufs=PSUM_BANKS))
 
-        w_raw = resident.tile([P, GATES, C_TILES, C3], BF16)
+        w_raw = resident.tile([P, C_TILES, GATES, C3], BF16)
         x_raw = [
-            resident.tile([P, PASSES, PACK, N_TILE], BF16, name="x_raw%d" % n)
-            for n in range(N_TILES)
+            [
+                [resident.tile([P, PACK, HALF], BF16, name="x_raw%d%d%d" % (b, g, half)) for half in range(HALVES)]
+                for g in range(PASSES)
+            ]
+            for b in range(BATCH)
         ]
-        m_sb = [
-            resident.tile([P, C_TILES, N_TILE], BF16, name="m_sb%d" % n) for n in range(N_TILES)
+        m_sb = [resident.tile([P, C_TILES, PIXELS], BF16, name="m_sb%d" % b) for b in range(BATCH)]
+        w_codes = [
+            resident.tile([P, ROW_CHUNKS * P], U32, name="w_codes%d" % r, align_bytes=64)
+            for r in range(C_TILES)
         ]
-        w_codes = resident.tile([P, W_CHUNKS * P], U32, align_bytes=64)
-        w_scales = resident.tile([P, W_CHUNKS * P], U8, align_bytes=64)
+        w_scales = [
+            resident.tile([P, ROW_CHUNKS * P], U8, name="w_scales%d" % r, align_bytes=64)
+            for r in range(C_TILES)
+        ]
         x_codes = [
-            resident.tile([P, PASSES * N_TILE], U32, name="x_codes%d" % n, align_bytes=64)
-            for n in range(N_TILES)
+            resident.tile([P, PASSES * PIXELS], U32, name="x_codes%d" % b, align_bytes=64)
+            for b in range(BATCH)
         ]
         x_scales = [
-            resident.tile([P, PASSES * N_TILE], U8, name="x_scales%d" % n, align_bytes=64)
-            for n in range(N_TILES)
+            resident.tile([P, PASSES * PIXELS], U8, name="x_scales%d" % b, align_bytes=64)
+            for b in range(BATCH)
         ]
 
-        def load_w(a, first_tile):
-            tiles = slice(first_tile, first_tile + 2)
-            nc.sync.dma_start(out=w_raw[:, a, tiles, :], in_=w_tiles[a][:, tiles, :])
+        def load_w(r, which=GATE_ORDER):
+            for a in which:
+                nc.sync.dma_start(out=w_raw[:, r, a, :], in_=w_tiles[a][:, r, :])
 
-        def load_x(n):
-            b, cols = pixels_of(n)
+        def load_x(b, half):
             for g in range(PASSES):
                 nc.sync.dma_start(
-                    out=x_raw[n][:, g, :, :],
-                    in_=pass_rows(b, g)[:, cols].rearrange("(p t) w -> p t w", t=PACK),
+                    out=x_raw[b][g][half][:],
+                    in_=pass_rows(b, g)[:, pixels(half)].rearrange("(p t) w -> p t w", t=PACK),
                 )
 
-        def load_m(n):
-            b, cols = pixels_of(n)
-            nc.sync.dma_start(out=m_sb[n][:], in_=m_tiles[b][:, :, cols])
+        def load_m(b, r):
+            nc.sync.dma_start(out=m_sb[b][:, r, :], in_=m_tiles[b][:, r, :])
 
-        bias_in = consts.tile([P, GATES, C_TILES], BF16)
-        nc.scalar.dma_start(out=bias_in[:], in_=bm.rearrange("(a q r) -> q a r", a=GATES, r=C_TILES))
-        for a in range(GATES):
-            for first_tile in range(0, C_TILES, 2):
-                load_w(a, first_tile)
-        for n in range(N_TILES):
-            load_x(n)
-            load_m(n)
+        bias = consts.tile([P, GATES, C_TILES], BF16)
+        load_w(0, GATE_ORDER[:1])
+        load_x(0, 0)
+        load_w(0, GATE_ORDER[1:])
+        nc.sync.dma_start(out=bias[:], in_=bm.rearrange("(a q r) -> q a r", a=GATES, r=C_TILES))
+        load_m(0, 0)
+        load_w(1)
+        load_m(0, 1)
+        load_x(0, 1)
+        load_w(2)
+        load_m(0, 2)
+        load_x(1, 0)
+        load_m(1, 0)
+        load_m(1, 1)
+        load_w(3)
+        load_m(1, 2)
+        load_m(0, 3)
+        load_x(1, 1)
+        load_m(1, 3)
 
         warm = consts.tile([P, 1], F32)
         nc.vector.memset(warm[:], 0.0)
@@ -112,132 +128,156 @@ def tile_self_attention_memory_module_pb_kernel(tc, z, h, m, Wm, bm, out_0, out_
         ident = consts.tile([P, P], F32)
         make_identity(nc, ident[:])
 
-        bias = consts.tile([P, GATES, C_TILES], F32)
-        nc.vector.tensor_copy(out=bias[:], in_=bias_in[:])
-
-        def chunk_of(a, r, g):
-            return (a * C_TILES + r) * PASSES + g
-
-        def turn_w_bank(j):
-            w_turned = psum.tile([P, CHUNKS_PER_BANK, 2, P], F32, tag="bank")
-            for s in range(CHUNKS_PER_BANK):
-                row_tile, g = divmod(j * CHUNKS_PER_BANK + s, PASSES)
-                a, r = divmod(row_tile, C_TILES)
-                words = w_raw[:, a, r, :].bitcast(F32)
-                for u in range(2):
-                    every_second = slice(g * 2 * P + u, (g + 1) * 2 * P, 2)
-                    nc.tensor.transpose(w_turned[:, s, u, :], words[:, every_second], ident[:])
-            w_grouped = stage.tile([P, CHUNKS_PER_BANK * P * PACK], BF16, align_bytes=64)
-            nc.scalar.copy(
-                out=w_grouped[:].bitcast(F32).rearrange("p (s o u) -> p s o u", s=CHUNKS_PER_BANK, u=2),
-                in_=w_turned[:].rearrange("p s u o -> p s o u"),
-            )
-            return w_grouped
-
-        def quantise_w(j, w_grouped):
-            cols = slice(j * CHUNKS_PER_BANK * P, (j + 1) * CHUNKS_PER_BANK * P)
-            nc.vector.quantize_mx(
-                out=w_codes[:, cols].bitcast(FP8X4), scales=w_scales[:, cols], in_=w_grouped[:]
-            )
-
-        def regroup_x(n, g):
-            copy = nc.vector.tensor_copy if n < HALVES else nc.scalar.copy
-            x_grouped = stage.tile([P, N_TILE, PACK], BF16, align_bytes=64)
-            copy(
-                out=x_grouped[:].rearrange("p (c i) t -> p c t i", i=RUN),
-                in_=x_raw[n][:, g, :, :].rearrange("p t (c i) -> p c t i", i=RUN),
-            )
-            return x_grouped
-
-        def quantise_x(n, g, x_grouped):
-            cols = slice(g * N_TILE, (g + 1) * N_TILE)
-            nc.vector.quantize_mx(
-                out=x_codes[n][:, cols].bitcast(FP8X4),
-                scales=x_scales[n][:, cols],
-                in_=x_grouped[:].rearrange("p w t -> p (w t)"),
-            )
-
-        def multiply(n, r, a):
-            acc = psum.tile([P, N_TILE], F32, tag="bank")
-            for g in range(PASSES):
-                w_cols = slice(chunk_of(a, r, g) * P, (chunk_of(a, r, g) + 1) * P)
-                x_cols = slice(g * N_TILE, (g + 1) * N_TILE)
-                nc.tensor.matmul_mx(
-                    out=acc[:],
-                    lhsT=w_codes[:, w_cols].bitcast(FP8X4),
-                    lhsT_scale=w_scales[:, w_cols],
-                    rhs=x_codes[n][:, x_cols].bitcast(FP8X4),
-                    rhs_scale=x_scales[n][:, x_cols],
-                    start=(g == 0),
-                    stop=(g == PASSES - 1),
+        def turn_w(r, first, count):
+            grouped = stage.tile([P, W_GROUP * P * PACK], BF16, name="w_grouped", align_bytes=64)
+            width = P * PACK
+            for offset in range(0, count, CHUNKS_PER_BANK):
+                chunks = range(offset, min(offset + CHUNKS_PER_BANK, count))
+                turned = psum.tile([P, CHUNKS_PER_BANK, 2, P], F32, tag="bank")
+                for s, chunk in enumerate(chunks):
+                    place, g = divmod(first + chunk, PASSES)
+                    words = w_raw[:, r, GATE_ORDER[place], :].bitcast(F32)
+                    for u in range(2):
+                        every_second = slice(g * 2 * P + u, (g + 1) * 2 * P, 2)
+                        nc.tensor.transpose(turned[:, s, u, :], words[:, every_second], ident[:])
+                columns = grouped[:, chunks.start * width : chunks.stop * width]
+                nc.scalar.copy(
+                    out=columns.bitcast(F32).rearrange("p (s o u) -> p s o u", s=len(chunks), u=2),
+                    in_=turned[:, : len(chunks), :, :].rearrange("p s u o -> p s o u"),
                 )
-            return acc
+            return r, first, count, grouped
 
-        def squash(acc, func, r, a, name):
-            result = gates.tile([P, N_TILE], F32, name=name)
-            nc.scalar.activation(out=result[:], in_=acc[:], func=func, bias=bias[:, a, r : r + 1], scale=1.0)
-            return result
+        def quantise_w(r, first, count, grouped):
+            cols = slice(first * P, (first + count) * P)
+            nc.vector.quantize_mx(
+                out=w_codes[r][:, cols].bitcast(FP8X4),
+                scales=w_scales[r][:, cols],
+                in_=grouped[:, : count * P * PACK],
+            )
 
-        def gates_of(n, r):
-            acc_g = multiply(n, r, CANDIDATE)
-            acc_i = multiply(n, r, IN_GATE)
-            acc_o = multiply(n, r, OUT_GATE)
-            return {
-                "n": n,
-                "r": r,
-                "cand": squash(acc_g, ACT.Tanh, r, CANDIDATE, "cand"),
-                "gate_i": squash(acc_i, ACT.Sigmoid, r, IN_GATE, "gate_i"),
-                "gate_o": squash(acc_o, ACT.Sigmoid, r, OUT_GATE, "gate_o"),
-            }
+        def prepare_w(r, group):
+            counts = [(first, min(group, ROW_CHUNKS - first)) for first in range(0, ROW_CHUNKS, group)]
+            for piece in [turn_w(r, first, count) for first, count in counts]:
+                quantise_w(*piece)
 
-        def difference(unit):
-            nc.vector.tensor_sub(out=unit["cand"][:], in0=unit["cand"][:], in1=m_sb[unit["n"]][:, unit["r"], :])
+        def prepare_x(b, g, half, copy):
+            grouped = stage.tile([P, HALF, PACK], BF16, name="x_grouped", align_bytes=64)
+            copy(
+                out=grouped[:].rearrange("p (c i) t -> p c t i", i=RUN),
+                in_=x_raw[b][g][half][:].rearrange("p t (c i) -> p c t i", i=RUN),
+            )
+            codes = slice(g * PIXELS + half * HALF, g * PIXELS + (half + 1) * HALF)
+            nc.vector.quantize_mx(
+                out=x_codes[b][:, codes].bitcast(FP8X4),
+                scales=x_scales[b][:, codes],
+                in_=grouped[:].rearrange("p w t -> p (w t)"),
+            )
 
-        def gated_step(unit):
-            nc.vector.tensor_mul(out=unit["cand"][:], in0=unit["gate_i"][:], in1=unit["cand"][:])
+        def multiply(acc, b, r, half, place, g):
+            first_w = (place * PASSES + g) * P
+            first_x = g * PIXELS + half * HALF
+            nc.tensor.matmul_mx(
+                out=acc[:],
+                lhsT=w_codes[r][:, first_w : first_w + P].bitcast(FP8X4),
+                lhsT_scale=w_scales[r][:, first_w : first_w + P],
+                rhs=x_codes[b][:, first_x : first_x + HALF].bitcast(FP8X4),
+                rhs_scale=x_scales[b][:, first_x : first_x + HALF],
+                start=(g == 0),
+                stop=(g == PASSES - 1),
+            )
 
-        def store(tiles, unit, result):
-            b, cols = pixels_of(unit["n"])
-            nc.sync.dma_start(out=tiles[b][:, unit["r"], cols], in_=result[:])
+        def squash(acc, gate, r, place, column):
+            a = GATE_ORDER[place]
+            nc.scalar.activation(
+                out=gate[:, column : column + HALF],
+                in_=acc[:],
+                func=ACT.Tanh if a == CANDIDATE else ACT.Sigmoid,
+                bias=bias[:, a, r : r + 1],
+                scale=1.0,
+            )
 
-        def new_memory(unit):
-            new_m = gates.tile([P, N_TILE], F32, name="new_m")
-            nc.vector.tensor_add(out=new_m[:], in0=unit["cand"][:], in1=m_sb[unit["n"]][:, unit["r"], :])
-            store(new_m_tiles, unit, new_m)
-            return new_m
+        def new_block(b, tiles, halves):
+            names = ("cand", "gate_i", "gate_o", "new_m")
+            block = {name: gates.tile([P, BLOCK], F32, name=name) for name in names}
+            block["place"] = (b, slice(tiles[0], tiles[-1] + 1), pixels(halves[0], len(halves)))
+            block["count"] = len(tiles)
+            block["size"] = len(tiles) * len(halves) * HALF
+            return block
 
-        def new_hidden(unit, new_m):
-            nc.vector.tensor_mul(out=unit["gate_o"][:], in0=unit["gate_o"][:], in1=new_m[:])
-            store(new_h_tiles, unit, unit["gate_o"])
+        def values(block, name):
+            return block[name][:, : block["size"]].rearrange("p (r w) -> p r w", r=block["count"])
 
-        copied = None
-        for j in range(W_BANKS):
-            w_grouped = turn_w_bank(j)
-            if copied is not None:
-                quantise_w(*copied)
-            copied = (j, w_grouped)
-        quantise_w(*copied)
-        copied = None
+        def memory(block):
+            b, tiles, cols = block["place"]
+            return m_sb[b][:, tiles, cols]
+
+        def store(out_tiles, block, name):
+            b, tiles, cols = block["place"]
+            nc.sync.dma_start(out=out_tiles[b][:, tiles, cols], in_=values(block, name))
+
+        def difference(block):
+            cand = values(block, "cand")
+            nc.vector.tensor_sub(out=cand, in0=cand, in1=memory(block))
+
+        def gated_step(block):
+            cand = values(block, "cand")
+            nc.vector.tensor_mul(out=cand, in0=values(block, "gate_i"), in1=cand)
+
+        def new_memory(block):
+            nc.vector.tensor_add(out=values(block, "new_m"), in0=values(block, "cand"), in1=memory(block))
+            store(new_m_tiles, block, "new_m")
+
+        def new_hidden(block):
+            gate_o = values(block, "gate_o")
+            nc.vector.tensor_mul(out=gate_o, in0=gate_o, in1=values(block, "new_m"))
+            store(new_h_tiles, block, "gate_o")
+
+        vector, scalar = nc.vector.tensor_copy, nc.scalar.copy
+
+        def prepare(what, *where):
+            if what == "w":
+                prepare_w(where[0], W_GROUP)
+            else:
+                b, half, copies = where
+                for g, copy in enumerate(copies):
+                    prepare_x(b, g, half, copy)
+
+        plan = [
+            (0, (0,), (0,), [("w", 1), ("x", 0, 1, (vector, scalar, scalar))]),
+            (0, (1,), (0,), [("w", 2)]),
+            (0, (0, 1), (1,), [("x", 1, 0, (vector, scalar, scalar))]),
+            (0, (2,), (0, 1), [("w", 3)]),
+            (1, (0, 1), (0,), [("x", 1, 1, (vector, scalar, scalar))]),
+            (1, (2,), (0,), []),
+            (0, (3,), (0, 1), []),
+            (1, (3,), (0,), []),
+            (1, (0, 1), (1,), []),
+            (1, (2,), (1,), []),
+            (1, (3,), (1,), []),
+        ]
+
+        prepare_w(0, CHUNKS_PER_BANK)
         for g in range(PASSES):
-            x_grouped = regroup_x(0, g)
-            if copied is not None:
-                quantise_x(*copied)
-            copied = (0, g, x_grouped)
-
+            prepare_x(0, g, 0, vector)
         earlier = None
-        for n in range(N_TILES):
-            for r in range(C_TILES):
-                if copied is not None:
-                    quantise_x(*copied)
-                    copied = None
-                unit = gates_of(n, r)
-                if n + 1 < N_TILES and r < PASSES:
-                    copied = (n + 1, r, regroup_x(n + 1, r))
-                difference(unit)
-                if earlier is not None:
-                    new_m = new_memory(earlier)
-                gated_step(unit)
-                if earlier is not None:
-                    new_hidden(earlier, new_m)
-                earlier = unit
-        new_hidden(earlier, new_memory(earlier))
+        for b, tiles, halves, ahead in plan:
+            block = new_block(b, tiles, halves)
+            outputs = [(r, half) for r in tiles for half in halves]
+            for place, name in enumerate(("cand", "gate_i", "gate_o")):
+                for i, (r, half) in enumerate(outputs):
+                    acc = psum.tile([P, HALF], F32, tag="bank", name="acc")
+                    for g in range(PASSES):
+                        multiply(acc, b, r, half, place, g)
+                    squash(acc, block[name], r, place, i * HALF)
+                if place == 1:
+                    for item in ahead:
+                        prepare(*item)
+            difference(block)
+            if earlier is not None:
+                new_memory(earlier)
+            gated_step(block)
+            if earlier is not None:
+                new_hidden(earlier)
+            earlier = block
+        new_memory(earlier)
+        new_hidden(earlier)

@@ -155,10 +155,8 @@ def tile_self_attention_memory_module_pb_kernel(tc, z, h, m, Wm, bm, out_0, out_
                 in_=grouped[:, : count * P * PACK],
             )
 
-        def prepare_w(r, group):
-            counts = [(first, min(group, ROW_CHUNKS - first)) for first in range(0, ROW_CHUNKS, group)]
-            for piece in [turn_w(r, first, count) for first, count in counts]:
-                quantise_w(*piece)
+        def chunk_groups(size):
+            return [(first, min(size, ROW_CHUNKS - first)) for first in range(0, ROW_CHUNKS, size)]
 
         def prepare_x(b, g, half, copy):
             grouped = stage.tile([P, HALF, PACK], BF16, name="x_grouped", align_bytes=64)
@@ -232,35 +230,27 @@ def tile_self_attention_memory_module_pb_kernel(tc, z, h, m, Wm, bm, out_0, out_
             nc.vector.tensor_mul(out=gate_o, in0=gate_o, in1=values(block, "new_m"))
             store(new_h_tiles, block, "gate_o")
 
-        vector, scalar = nc.vector.tensor_copy, nc.scalar.copy
-
-        def prepare(what, *where):
-            if what == "w":
-                prepare_w(where[0], W_GROUP)
-            else:
-                b, half, copies = where
-                for g, copy in enumerate(copies):
-                    prepare_x(b, g, half, copy)
-
+        on_vector, on_scalar = nc.vector.tensor_copy, nc.scalar.copy
         plan = [
-            (0, (0,), (0,), [("w", 1), ("x", 0, 1, (vector, scalar, scalar))]),
-            (0, (1,), (0,), [("w", 2)]),
-            (0, (0, 1), (1,), [("x", 1, 0, (vector, scalar, scalar))]),
-            (0, (2,), (0, 1), [("w", 3)]),
-            (1, (0, 1), (0,), [("x", 1, 1, (vector, scalar, scalar))]),
-            (1, (2,), (0,), []),
-            (0, (3,), (0, 1), []),
-            (1, (3,), (0,), []),
-            (1, (0, 1), (1,), []),
-            (1, (2,), (1,), []),
-            (1, (3,), (1,), []),
+            (0, (0,), (0,), 1, (0, 1)),
+            (0, (1,), (0,), 2, None),
+            (0, (0, 1), (1,), None, (1, 0)),
+            (0, (2,), (0, 1), 3, None),
+            (1, (0, 1), (0,), None, (1, 1)),
+            (1, (2,), (0,), None, None),
+            (0, (3,), (0, 1), None, None),
+            (1, (3,), (0,), None, None),
+            (1, (0, 1), (1,), None, None),
+            (1, (2,), (1,), None, None),
+            (1, (3,), (1,), None, None),
         ]
 
-        prepare_w(0, CHUNKS_PER_BANK)
+        for piece in [turn_w(0, first, count) for first, count in chunk_groups(CHUNKS_PER_BANK)]:
+            quantise_w(*piece)
         for g in range(PASSES):
-            prepare_x(0, g, 0, vector)
+            prepare_x(0, g, 0, on_vector)
         earlier = None
-        for b, tiles, halves, ahead in plan:
+        for b, tiles, halves, next_tile, next_half in plan:
             block = new_block(b, tiles, halves)
             outputs = [(r, half) for r in tiles for half in halves]
             for place, name in enumerate(("cand", "gate_i", "gate_o")):
@@ -269,9 +259,10 @@ def tile_self_attention_memory_module_pb_kernel(tc, z, h, m, Wm, bm, out_0, out_
                     for g in range(PASSES):
                         multiply(acc, b, r, half, place, g)
                     squash(acc, block[name], r, place, i * HALF)
-                if place == 1:
-                    for item in ahead:
-                        prepare(*item)
+                if next_tile is not None:
+                    quantise_w(*turn_w(next_tile, *chunk_groups(W_GROUP)[place]))
+                if next_half is not None:
+                    prepare_x(next_half[0], place, next_half[1], on_scalar if place > 0 else on_vector)
             difference(block)
             if earlier is not None:
                 new_memory(earlier)

@@ -57,17 +57,11 @@ def tile_self_attention_memory_module_pb_kernel(tc, z, h, m, Wm, bm, out_0, out_
         consts = ctx.enter_context(tc.tile_pool(name="consts", bufs=1))
         resident = ctx.enter_context(tc.tile_pool(name="resident", bufs=1))
         stage = ctx.enter_context(tc.tile_pool(name="stage", bufs=4))
+        raw = ctx.enter_context(tc.tile_pool(name="raw", bufs=2))
         gates = ctx.enter_context(tc.tile_pool(name="gates", bufs=3))
+        results = ctx.enter_context(tc.tile_pool(name="results", bufs=5))
         psum = ctx.enter_context(tc.psum_pool(name="psum", bufs=PSUM_BANKS))
 
-        w_raw = resident.tile([P, C_TILES, GATES, C3], BF16)
-        x_raw = [
-            [
-                [resident.tile([P, PACK, HALF], BF16, name="x_raw%d%d%d" % (b, g, half)) for half in range(HALVES)]
-                for g in range(PASSES)
-            ]
-            for b in range(BATCH)
-        ]
         m_sb = [resident.tile([P, C_TILES, PIXELS], BF16, name="m_sb%d" % b) for b in range(BATCH)]
         w_codes = [
             resident.tile([P, ROW_CHUNKS * P], U32, name="w_codes%d" % r, align_bytes=64)
@@ -86,14 +80,19 @@ def tile_self_attention_memory_module_pb_kernel(tc, z, h, m, Wm, bm, out_0, out_
             for b in range(BATCH)
         ]
 
+        w_raw, x_raw = {}, {}
+
         def load_w(r, which=GATE_ORDER):
+            if r not in w_raw:
+                w_raw[r] = raw.tile([P, GATES, C3], BF16, name="w_raw")
             for a in which:
-                nc.sync.dma_start(out=w_raw[:, r, a, :], in_=w_tiles[a][:, r, :])
+                nc.sync.dma_start(out=w_raw[r][:, a, :], in_=w_tiles[a][:, r, :])
 
         def load_x(b, half):
             for g in range(PASSES):
+                x_raw[b, g, half] = raw.tile([P, PACK, HALF], BF16, name="x_raw%d" % g)
                 nc.sync.dma_start(
-                    out=x_raw[b][g][half][:],
+                    out=x_raw[b, g, half][:],
                     in_=pass_rows(b, g)[:, pixels(half)].rearrange("(p t) w -> p t w", t=PACK),
                 )
 
@@ -109,16 +108,6 @@ def tile_self_attention_memory_module_pb_kernel(tc, z, h, m, Wm, bm, out_0, out_
         load_w(1)
         load_m(0, 1)
         load_x(0, 1)
-        load_w(2)
-        load_m(0, 2)
-        load_x(1, 0)
-        load_m(1, 0)
-        load_m(1, 1)
-        load_w(3)
-        load_m(1, 2)
-        load_m(0, 3)
-        load_x(1, 1)
-        load_m(1, 3)
 
         warm = consts.tile([P, 1], F32)
         nc.vector.memset(warm[:], 0.0)
@@ -136,7 +125,7 @@ def tile_self_attention_memory_module_pb_kernel(tc, z, h, m, Wm, bm, out_0, out_
                 turned = psum.tile([P, CHUNKS_PER_BANK, 2, P], F32, tag="bank")
                 for s, chunk in enumerate(chunks):
                     place, g = divmod(first + chunk, PASSES)
-                    words = w_raw[:, r, GATE_ORDER[place], :].bitcast(F32)
+                    words = w_raw[r][:, GATE_ORDER[place], :].bitcast(F32)
                     for u in range(2):
                         every_second = slice(g * 2 * P + u, (g + 1) * 2 * P, 2)
                         nc.tensor.transpose(turned[:, s, u, :], words[:, every_second], ident[:])
@@ -162,7 +151,7 @@ def tile_self_attention_memory_module_pb_kernel(tc, z, h, m, Wm, bm, out_0, out_
             grouped = stage.tile([P, HALF, PACK], BF16, name="x_grouped", align_bytes=64)
             copy(
                 out=grouped[:].rearrange("p (c i) t -> p c t i", i=RUN),
-                in_=x_raw[b][g][half][:].rearrange("p t (c i) -> p c t i", i=RUN),
+                in_=x_raw[b, g, half][:].rearrange("p t (c i) -> p c t i", i=RUN),
             )
             codes = slice(g * PIXELS + half * HALF, g * PIXELS + (half + 1) * HALF)
             nc.vector.quantize_mx(
@@ -195,8 +184,11 @@ def tile_self_attention_memory_module_pb_kernel(tc, z, h, m, Wm, bm, out_0, out_
             )
 
         def new_block(b, tiles, halves):
-            names = ("cand", "gate_i", "gate_o", "new_m")
-            block = {name: gates.tile([P, BLOCK], F32, name=name) for name in names}
+            block = {
+                "cand": results.tile([P, BLOCK], F32, name="cand"),
+                "gate_i": gates.tile([P, BLOCK], F32, name="gate_i"),
+                "gate_o": results.tile([P, BLOCK], F32, name="gate_o"),
+            }
             block["place"] = (b, slice(tiles[0], tiles[-1] + 1), pixels(halves[0], len(halves)))
             block["count"] = len(tiles)
             block["size"] = len(tiles) * len(halves) * HALF
@@ -222,35 +214,39 @@ def tile_self_attention_memory_module_pb_kernel(tc, z, h, m, Wm, bm, out_0, out_
             nc.vector.tensor_mul(out=cand, in0=values(block, "gate_i"), in1=cand)
 
         def new_memory(block):
-            nc.vector.tensor_add(out=values(block, "new_m"), in0=values(block, "cand"), in1=memory(block))
-            store(new_m_tiles, block, "new_m")
+            cand = values(block, "cand")
+            nc.vector.tensor_add(out=cand, in0=cand, in1=memory(block))
+            store(new_m_tiles, block, "cand")
 
         def new_hidden(block):
             gate_o = values(block, "gate_o")
-            nc.vector.tensor_mul(out=gate_o, in0=gate_o, in1=values(block, "new_m"))
+            nc.vector.tensor_mul(out=gate_o, in0=gate_o, in1=values(block, "cand"))
             store(new_h_tiles, block, "gate_o")
 
         on_vector, on_scalar = nc.vector.tensor_copy, nc.scalar.copy
         plan = [
-            (0, (0,), (0,), 1, (0, 1)),
-            (0, (1,), (0,), 2, None),
-            (0, (0, 1), (1,), None, (1, 0)),
-            (0, (2,), (0, 1), 3, None),
-            (1, (0, 1), (0,), None, (1, 1)),
-            (1, (2,), (0,), None, None),
-            (0, (3,), (0, 1), None, None),
-            (1, (3,), (0,), None, None),
-            (1, (0, 1), (1,), None, None),
-            (1, (2,), (1,), None, None),
-            (1, (3,), (1,), None, None),
+            (0, (0,), (0,), [("w", 2), ("m", 0, 2)], 1, (0, 1)),
+            (0, (1,), (0,), [("x", 1, 0), ("m", 1, 0), ("m", 1, 1)], 2, None),
+            (0, (0, 1), (1,), [("w", 3), ("m", 1, 2), ("m", 0, 3)], None, (1, 0)),
+            (0, (2,), (0, 1), [("x", 1, 1), ("m", 1, 3)], 3, None),
+            (1, (0, 1), (0,), [], None, (1, 1)),
+            (1, (2,), (0,), [], None, None),
+            (0, (3,), (0, 1), [], None, None),
+            (1, (3,), (0,), [], None, None),
+            (1, (0, 1), (1,), [], None, None),
+            (1, (2,), (1,), [], None, None),
+            (1, (3,), (1,), [], None, None),
         ]
+        load = {"w": load_w, "x": load_x, "m": load_m}
 
         for piece in [turn_w(0, first, count) for first, count in chunk_groups(CHUNKS_PER_BANK)]:
             quantise_w(*piece)
         for g in range(PASSES):
             prepare_x(0, g, 0, on_vector)
         earlier = None
-        for b, tiles, halves, next_tile, next_half in plan:
+        for b, tiles, halves, loads, next_tile, next_half in plan:
+            for what, *where in loads:
+                load[what](*where)
             block = new_block(b, tiles, halves)
             outputs = [(r, half) for r in tiles for half in halves]
             for place, name in enumerate(("cand", "gate_i", "gate_o")):

@@ -25,11 +25,8 @@ GATE_ORDER = (CANDIDATE, IN_GATE, OUT_GATE)
 C_TILES = C // P
 HALF = 512
 HALVES = PIXELS // HALF
-BLOCK = 2 * HALF
+X_TILES = BATCH * HALVES
 PSUM_BANKS = 8
-ROW_CHUNKS = GATES * PASSES
-CHUNKS_PER_BANK = 2
-W_GROUP = 4
 RUN = 4
 
 FLOPS = 2 * C3 * C3 * BATCH * PIXELS
@@ -45,226 +42,254 @@ def tile_self_attention_memory_module_pb_kernel(tc, z, h, m, Wm, bm, out_0, out_
     new_m_tiles = out_1.rearrange("b (q r) i j -> b q r (i j)", r=C_TILES)
     w_tiles = Wm.rearrange("(a q r) k -> a q r k", a=GATES, r=C_TILES)
 
+    def place_of(n):
+        b, half = divmod(n, HALVES)
+        return b, slice(half * HALF, (half + 1) * HALF)
+
     def pass_rows(b, g):
         if g < Z_PASSES:
             return z_rows[b, g * K_PASS : (g + 1) * K_PASS, :]
         return h_rows[b]
 
-    def pixels(first_half, halves=1):
-        return slice(first_half * HALF, (first_half + halves) * HALF)
-
     with ExitStack() as ctx:
-        consts = ctx.enter_context(tc.tile_pool(name="consts", bufs=1))
         resident = ctx.enter_context(tc.tile_pool(name="resident", bufs=1))
-        stage = ctx.enter_context(tc.tile_pool(name="stage", bufs=4))
-        raw = ctx.enter_context(tc.tile_pool(name="raw", bufs=2))
+        stage = ctx.enter_context(tc.tile_pool(name="stage", bufs=5))
         gates = ctx.enter_context(tc.tile_pool(name="gates", bufs=3))
-        results = ctx.enter_context(tc.tile_pool(name="results", bufs=5))
+        results = ctx.enter_context(tc.tile_pool(name="results", bufs=8))
         psum = ctx.enter_context(tc.psum_pool(name="psum", bufs=PSUM_BANKS))
 
+        warm = resident.tile([P, 1], F32)
+        nc.vector.memset(warm[:], 0.0)
+        warm_out = resident.tile([P, 1], F32)
+        nc.scalar.activation(out=warm_out[:], in_=warm[:], func=ACT.Sigmoid)
+
+        ident = resident.tile([P, P], F32)
+        make_identity(nc, ident[:])
+
+        ctx.enter_context(tc.manual_schedule())
+
+        bias = resident.tile([P, GATES, C_TILES], BF16)
+        w_raw = [resident.tile([P, GATES, C3], BF16, name="w_raw%d" % r) for r in range(C_TILES)]
+        x_raw = [
+            [resident.tile([P, PACK, HALF], BF16, name="x_raw%d%d" % (n, g)) for g in range(PASSES)]
+            for n in range(X_TILES)
+        ]
         m_sb = [resident.tile([P, C_TILES, PIXELS], BF16, name="m_sb%d" % b) for b in range(BATCH)]
         w_codes = [
-            resident.tile([P, ROW_CHUNKS * P], U32, name="w_codes%d" % r, align_bytes=64)
+            resident.tile([P, GATES * PASSES * P], U32, name="w_codes%d" % r, align_bytes=64)
             for r in range(C_TILES)
         ]
         w_scales = [
-            resident.tile([P, ROW_CHUNKS * P], U8, name="w_scales%d" % r, align_bytes=64)
+            resident.tile([P, GATES * PASSES * P], U8, name="w_scales%d" % r, align_bytes=64)
             for r in range(C_TILES)
         ]
         x_codes = [
-            resident.tile([P, PASSES * PIXELS], U32, name="x_codes%d" % b, align_bytes=64)
-            for b in range(BATCH)
+            resident.tile([P, PASSES * HALF], U32, name="x_codes%d" % n, align_bytes=64)
+            for n in range(X_TILES)
         ]
         x_scales = [
-            resident.tile([P, PASSES * PIXELS], U8, name="x_scales%d" % b, align_bytes=64)
-            for b in range(BATCH)
+            resident.tile([P, PASSES * HALF], U8, name="x_scales%d" % n, align_bytes=64)
+            for n in range(X_TILES)
         ]
 
-        w_raw, x_raw = {}, {}
-
         def load_w(r, which=GATE_ORDER):
-            if r not in w_raw:
-                w_raw[r] = raw.tile([P, GATES, C3], BF16, name="w_raw")
             for a in which:
                 nc.sync.dma_start(out=w_raw[r][:, a, :], in_=w_tiles[a][:, r, :])
 
-        def load_x(b, half):
+        def load_x(n):
+            b, cols = place_of(n)
             for g in range(PASSES):
-                x_raw[b, g, half] = raw.tile([P, PACK, HALF], BF16, name="x_raw%d" % g)
                 nc.sync.dma_start(
-                    out=x_raw[b, g, half][:],
-                    in_=pass_rows(b, g)[:, pixels(half)].rearrange("(p t) w -> p t w", t=PACK),
+                    out=x_raw[n][g][:],
+                    in_=pass_rows(b, g)[:, cols].rearrange("(p t) w -> p t w", t=PACK),
                 )
 
         def load_m(b, r):
             nc.sync.dma_start(out=m_sb[b][:, r, :], in_=m_tiles[b][:, r, :])
 
-        bias = consts.tile([P, GATES, C_TILES], BF16)
         load_w(0, GATE_ORDER[:1])
-        load_x(0, 0)
+        load_x(0)
         load_w(0, GATE_ORDER[1:])
         nc.sync.dma_start(out=bias[:], in_=bm.rearrange("(a q r) -> q a r", a=GATES, r=C_TILES))
         load_m(0, 0)
         load_w(1)
         load_m(0, 1)
-        load_x(0, 1)
+        load_x(1)
+        load_w(2)
+        load_m(0, 2)
+        load_x(2)
+        load_m(1, 0)
+        load_m(1, 1)
+        load_w(3)
+        load_m(1, 2)
+        load_m(0, 3)
+        load_x(3)
+        load_m(1, 3)
 
-        warm = consts.tile([P, 1], F32)
-        nc.vector.memset(warm[:], 0.0)
-        warm_out = consts.tile([P, 1], F32)
-        nc.scalar.activation(out=warm_out[:], in_=warm[:], func=ACT.Sigmoid)
-
-        ident = consts.tile([P, P], F32)
-        make_identity(nc, ident[:])
-
-        def turn_w(r, first, count):
-            grouped = stage.tile([P, W_GROUP * P * PACK], BF16, name="w_grouped", align_bytes=64)
-            width = P * PACK
-            for offset in range(0, count, CHUNKS_PER_BANK):
-                chunks = range(offset, min(offset + CHUNKS_PER_BANK, count))
-                turned = psum.tile([P, CHUNKS_PER_BANK, 2, P], F32, tag="bank")
-                for s, chunk in enumerate(chunks):
-                    place, g = divmod(first + chunk, PASSES)
-                    words = w_raw[r][:, GATE_ORDER[place], :].bitcast(F32)
-                    for u in range(2):
-                        every_second = slice(g * 2 * P + u, (g + 1) * 2 * P, 2)
-                        nc.tensor.transpose(turned[:, s, u, :], words[:, every_second], ident[:])
-                columns = grouped[:, chunks.start * width : chunks.stop * width]
-                nc.scalar.copy(
-                    out=columns.bitcast(F32).rearrange("p (s o u) -> p s o u", s=len(chunks), u=2),
-                    in_=turned[:, : len(chunks), :, :].rearrange("p s u o -> p s o u"),
-                )
-            return r, first, count, grouped
-
-        def quantise_w(r, first, count, grouped):
-            cols = slice(first * P, (first + count) * P)
-            nc.vector.quantize_mx(
-                out=w_codes[r][:, cols].bitcast(FP8X4),
-                scales=w_scales[r][:, cols],
-                in_=grouped[:, : count * P * PACK],
+        def turn_w(r, place, passes):
+            count = len(passes)
+            turned = psum.tile([P, 2, 2, P], F32, tag="bank")
+            words = w_raw[r][:, GATE_ORDER[place], :].bitcast(F32)
+            for s, g in enumerate(passes):
+                for u in range(2):
+                    every_second = slice(g * 2 * P + u, (g + 1) * 2 * P, 2)
+                    nc.tensor.transpose(turned[:, s, u, :], words[:, every_second], ident[:])
+            grouped = stage.tile([P, 2 * P * PACK], BF16, name="w_grouped", align_bytes=64)
+            columns = grouped[:, : count * P * PACK]
+            nc.scalar.copy(
+                out=columns.bitcast(F32).rearrange("p (s o u) -> p s o u", s=count, u=2),
+                in_=turned[:, :count, :, :].rearrange("p s u o -> p s o u"),
             )
 
-        def chunk_groups(size):
-            return [(first, min(size, ROW_CHUNKS - first)) for first in range(0, ROW_CHUNKS, size)]
+            def quantise():
+                first = (place * PASSES + passes[0]) * P
+                cols = slice(first, first + count * P)
+                nc.vector.quantize_mx(
+                    out=w_codes[r][:, cols].bitcast(FP8X4), scales=w_scales[r][:, cols], in_=columns
+                )
 
-        def prepare_x(b, g, half, copy):
+            return quantise
+
+        def turn_gate(r, place):
+            return [turn_w(r, place, passes) for passes in ((0, 1), (2,))]
+
+        def regroup_x(n, g, copy):
             grouped = stage.tile([P, HALF, PACK], BF16, name="x_grouped", align_bytes=64)
             copy(
                 out=grouped[:].rearrange("p (c i) t -> p c t i", i=RUN),
-                in_=x_raw[b, g, half][:].rearrange("p t (c i) -> p c t i", i=RUN),
-            )
-            codes = slice(g * PIXELS + half * HALF, g * PIXELS + (half + 1) * HALF)
-            nc.vector.quantize_mx(
-                out=x_codes[b][:, codes].bitcast(FP8X4),
-                scales=x_scales[b][:, codes],
-                in_=grouped[:].rearrange("p w t -> p (w t)"),
+                in_=x_raw[n][g][:].rearrange("p t (c i) -> p c t i", i=RUN),
             )
 
-        def multiply(acc, b, r, half, place, g):
-            first_w = (place * PASSES + g) * P
-            first_x = g * PIXELS + half * HALF
-            nc.tensor.matmul_mx(
-                out=acc[:],
-                lhsT=w_codes[r][:, first_w : first_w + P].bitcast(FP8X4),
-                lhsT_scale=w_scales[r][:, first_w : first_w + P],
-                rhs=x_codes[b][:, first_x : first_x + HALF].bitcast(FP8X4),
-                rhs_scale=x_scales[b][:, first_x : first_x + HALF],
-                start=(g == 0),
-                stop=(g == PASSES - 1),
-            )
+            def quantise():
+                cols = slice(g * HALF, (g + 1) * HALF)
+                nc.vector.quantize_mx(
+                    out=x_codes[n][:, cols].bitcast(FP8X4),
+                    scales=x_scales[n][:, cols],
+                    in_=grouped[:].rearrange("p w t -> p (w t)"),
+                )
 
-        def squash(acc, gate, r, place, column):
+            return quantise
+
+        on_vector, on_scalar = nc.vector.tensor_copy, nc.scalar.copy
+
+        def regroup_later(n, g):
+            made = []
+
+            def regroup():
+                made.append(regroup_x(n, g, on_vector))
+
+            def quantise():
+                made[0]()
+
+            return [regroup, quantise]
+
+        def multiply(n, r, place):
+            acc = psum.tile([P, HALF], F32, tag="bank", name="acc")
+            for g in range(PASSES):
+                first_w = (place * PASSES + g) * P
+                x_cols = slice(g * HALF, (g + 1) * HALF)
+                nc.tensor.matmul_mx(
+                    out=acc[:],
+                    lhsT=w_codes[r][:, first_w : first_w + P].bitcast(FP8X4),
+                    lhsT_scale=w_scales[r][:, first_w : first_w + P],
+                    rhs=x_codes[n][:, x_cols].bitcast(FP8X4),
+                    rhs_scale=x_scales[n][:, x_cols],
+                    start=(g == 0),
+                    stop=(g == PASSES - 1),
+                )
+            return acc
+
+        def squash(acc, gate, r, place):
             a = GATE_ORDER[place]
             nc.scalar.activation(
-                out=gate[:, column : column + HALF],
+                out=gate[:],
                 in_=acc[:],
                 func=ACT.Tanh if a == CANDIDATE else ACT.Sigmoid,
                 bias=bias[:, a, r : r + 1],
                 scale=1.0,
             )
 
-        def new_block(b, tiles, halves):
-            block = {
-                "cand": results.tile([P, BLOCK], F32, name="cand"),
-                "gate_i": gates.tile([P, BLOCK], F32, name="gate_i"),
-                "gate_o": results.tile([P, BLOCK], F32, name="gate_o"),
+        def new_unit(n, r):
+            return {
+                "n": n,
+                "r": r,
+                "cand": results.tile([P, HALF], F32, name="cand"),
+                "gate_i": gates.tile([P, HALF], F32, name="gate_i"),
+                "gate_o": results.tile([P, HALF], F32, name="gate_o"),
             }
-            block["place"] = (b, slice(tiles[0], tiles[-1] + 1), pixels(halves[0], len(halves)))
-            block["count"] = len(tiles)
-            block["size"] = len(tiles) * len(halves) * HALF
-            return block
 
-        def values(block, name):
-            return block[name][:, : block["size"]].rearrange("p (r w) -> p r w", r=block["count"])
+        def memory(unit):
+            b, cols = place_of(unit["n"])
+            return m_sb[b][:, unit["r"], cols]
 
-        def memory(block):
-            b, tiles, cols = block["place"]
-            return m_sb[b][:, tiles, cols]
+        def store(out_tiles, unit, name):
+            b, cols = place_of(unit["n"])
+            nc.sync.dma_start(out=out_tiles[b][:, unit["r"], cols], in_=unit[name][:])
 
-        def store(out_tiles, block, name):
-            b, tiles, cols = block["place"]
-            nc.sync.dma_start(out=out_tiles[b][:, tiles, cols], in_=values(block, name))
+        def difference(unit):
+            nc.vector.tensor_sub(out=unit["cand"][:], in0=unit["cand"][:], in1=memory(unit))
 
-        def difference(block):
-            cand = values(block, "cand")
-            nc.vector.tensor_sub(out=cand, in0=cand, in1=memory(block))
+        def gated_step(unit):
+            nc.vector.tensor_mul(out=unit["cand"][:], in0=unit["gate_i"][:], in1=unit["cand"][:])
 
-        def gated_step(block):
-            cand = values(block, "cand")
-            nc.vector.tensor_mul(out=cand, in0=values(block, "gate_i"), in1=cand)
+        def new_memory(unit):
+            nc.vector.tensor_add(out=unit["cand"][:], in0=unit["cand"][:], in1=memory(unit))
+            store(new_m_tiles, unit, "cand")
 
-        def new_memory(block):
-            cand = values(block, "cand")
-            nc.vector.tensor_add(out=cand, in0=cand, in1=memory(block))
-            store(new_m_tiles, block, "cand")
+        def new_hidden(unit):
+            nc.vector.tensor_mul(out=unit["gate_o"][:], in0=unit["gate_o"][:], in1=unit["cand"][:])
+            store(new_h_tiles, unit, "gate_o")
 
-        def new_hidden(block):
-            gate_o = values(block, "gate_o")
-            nc.vector.tensor_mul(out=gate_o, in0=gate_o, in1=values(block, "cand"))
-            store(new_h_tiles, block, "gate_o")
+        first_gate = turn_gate(0, 0)
+        x_first = regroup_x(0, 0, on_vector)
+        x_second = regroup_x(0, 1, on_scalar)
+        first_gate[0]()
+        x_first()
+        first_gate[1]()
+        x_third = regroup_x(0, 2, on_vector)
+        x_second()
+        second_gate = turn_gate(0, 1)
+        x_third()
+        third_gate = turn_gate(0, 2)
+        for quantise in second_gate + third_gate:
+            quantise()
 
-        on_vector, on_scalar = nc.vector.tensor_copy, nc.scalar.copy
         plan = [
-            (0, (0,), (0,), [("w", 2), ("m", 0, 2)], 1, (0, 1)),
-            (0, (1,), (0,), [("x", 1, 0), ("m", 1, 0), ("m", 1, 1)], 2, None),
-            (0, (0, 1), (1,), [("w", 3), ("m", 1, 2), ("m", 0, 3)], None, (1, 0)),
-            (0, (2,), (0, 1), [("x", 1, 1), ("m", 1, 3)], 3, None),
-            (1, (0, 1), (0,), [], None, (1, 1)),
-            (1, (2,), (0,), [], None, None),
-            (0, (3,), (0, 1), [], None, None),
-            (1, (3,), (0,), [], None, None),
-            (1, (0, 1), (1,), [], None, None),
-            (1, (2,), (1,), [], None, None),
-            (1, (3,), (1,), [], None, None),
+            (0, 0, 1, [(1, 0, 0, on_vector), (1, 1, 1, on_vector), (1, 2, 2, on_vector)]),
+            (0, 1, 2, []),
+            (1, 0, None, [(2, 0, 0, on_vector), (2, 1, 0, on_scalar)]),
+            (1, 1, None, [(2, 2, 0, on_scalar)]),
+            (0, 2, None, []),
+            (1, 2, 3, []),
+            (2, 0, None, []),
+            (2, 1, None, [(3, 0, 0, on_vector)]),
+            (2, 2, None, [(3, 1, 0, on_scalar)]),
+            (0, 3, None, []),
+            (1, 3, None, [(3, 2, 0, on_scalar)]),
+            (2, 3, None, []),
+            (3, 0, None, []),
+            (3, 1, None, []),
+            (3, 2, None, []),
+            (3, 3, None, []),
         ]
-        load = {"w": load_w, "x": load_x, "m": load_m}
-
-        for piece in [turn_w(0, first, count) for first, count in chunk_groups(CHUNKS_PER_BANK)]:
-            quantise_w(*piece)
-        for g in range(PASSES):
-            prepare_x(0, g, 0, on_vector)
         earlier = None
-        for b, tiles, halves, loads, next_tile, next_half in plan:
-            for what, *where in loads:
-                load[what](*where)
-            block = new_block(b, tiles, halves)
-            outputs = [(r, half) for r in tiles for half in halves]
+        for n, r, next_tile, x_passes in plan:
+            unit = new_unit(n, r)
+            extras = []
             for place, name in enumerate(("cand", "gate_i", "gate_o")):
-                for i, (r, half) in enumerate(outputs):
-                    acc = psum.tile([P, HALF], F32, tag="bank", name="acc")
-                    for g in range(PASSES):
-                        multiply(acc, b, r, half, place, g)
-                    squash(acc, block[name], r, place, i * HALF)
+                squash(multiply(n, r, place), unit[name], r, place)
                 if next_tile is not None:
-                    quantise_w(*turn_w(next_tile, *chunk_groups(W_GROUP)[place]))
-                if next_half is not None:
-                    prepare_x(next_half[0], place, next_half[1], on_scalar if place > 0 else on_vector)
-            difference(block)
-            if earlier is not None:
-                new_memory(earlier)
-            gated_step(block)
-            if earlier is not None:
-                new_hidden(earlier)
-            earlier = block
+                    extras += turn_gate(next_tile, place)
+                for x_tile, g, behind, copy in x_passes:
+                    if behind == place:
+                        extras += [regroup_x(x_tile, g, copy)] if copy is on_scalar else regroup_later(x_tile, g)
+            steps = [(difference, unit), (new_memory, earlier), (gated_step, unit), (new_hidden, earlier)]
+            bounds = [(len(extras) * j + len(steps) - 1) // len(steps) for j in range(len(steps) + 1)]
+            for j, (step, of_unit) in enumerate(steps):
+                if of_unit is not None:
+                    step(of_unit)
+                for extra in extras[bounds[j] : bounds[j + 1]]:
+                    extra()
+            earlier = unit
         new_memory(earlier)
         new_hidden(earlier)

@@ -226,6 +226,9 @@ def tile_self_attention_memory_module_pb_kernel(tc, z, h, m, Wm, bm, out_0, out_
             b, cols = place_of(unit["n"])
             nc.sync.dma_start(out=out_tiles[b][:, unit["r"], cols], in_=unit[name][:])
 
+        def no_step(unit):
+            pass
+
         def difference(unit):
             nc.vector.tensor_sub(out=unit["cand"][:], in0=unit["cand"][:], in1=memory(unit))
 
@@ -250,22 +253,21 @@ def tile_self_attention_memory_module_pb_kernel(tc, z, h, m, Wm, bm, out_0, out_
         x_second()
         second_gate = turn_gate(0, 1)
         x_third()
-        third_gate = turn_gate(0, 2)
-        for quantise in second_gate + third_gate:
+        for quantise in second_gate:
             quantise()
 
         plan = [
-            (0, 0, 1, [(1, 0, 0, on_vector), (1, 1, 1, on_vector), (1, 2, 2, on_vector)]),
+            (0, 0, 1, [(1, 0, 0, on_vector), (1, 1, 1, on_vector), (1, 2, 2, on_scalar)]),
             (0, 1, 2, []),
-            (1, 0, None, [(2, 0, 0, on_vector), (2, 1, 0, on_scalar)]),
-            (1, 1, None, [(2, 2, 0, on_scalar)]),
-            (0, 2, None, []),
-            (1, 2, 3, []),
-            (2, 0, None, []),
-            (2, 1, None, [(3, 0, 0, on_vector)]),
-            (2, 2, None, [(3, 1, 0, on_scalar)]),
+            (1, 0, None, [(2, 0, 0, on_vector), (2, 1, 1, on_vector), (2, 2, 2, on_scalar)]),
+            (1, 1, None, []),
+            (0, 2, 3, []),
+            (1, 2, None, [(3, 0, 0, on_vector)]),
+            (2, 0, None, [(3, 1, 0, on_scalar)]),
+            (2, 1, None, [(3, 2, 0, on_scalar)]),
+            (2, 2, None, []),
             (0, 3, None, []),
-            (1, 3, None, [(3, 2, 0, on_scalar)]),
+            (1, 3, None, []),
             (2, 3, None, []),
             (3, 0, None, []),
             (3, 1, None, []),
@@ -278,16 +280,22 @@ def tile_self_attention_memory_module_pb_kernel(tc, z, h, m, Wm, bm, out_0, out_
             extras = []
             for place, name in enumerate(("cand", "gate_i", "gate_o")):
                 squash(multiply(n, r, place), unit[name], r, place)
+                if earlier is None and place == 0:
+                    third_gate = turn_gate(0, 2)
+                    difference(unit)
+                    for quantise in third_gate:
+                        quantise()
                 if next_tile is not None:
                     extras += turn_gate(next_tile, place)
                 for x_tile, g, behind, copy in x_passes:
                     if behind == place:
                         extras += [regroup_x(x_tile, g, copy)] if copy is on_scalar else regroup_later(x_tile, g)
             steps = [(difference, unit), (new_memory, earlier), (gated_step, unit), (new_hidden, earlier)]
+            if earlier is None:
+                steps = [(no_step, unit), (no_step, unit), (gated_step, unit), (no_step, unit)]
             bounds = [(len(extras) * j + len(steps) - 1) // len(steps) for j in range(len(steps) + 1)]
             for j, (step, of_unit) in enumerate(steps):
-                if of_unit is not None:
-                    step(of_unit)
+                step(of_unit)
                 for extra in extras[bounds[j] : bounds[j + 1]]:
                     extra()
             earlier = unit

@@ -25,7 +25,8 @@ GATE_ORDER = (CANDIDATE, IN_GATE, OUT_GATE)
 C_TILES = C // P
 HALF = 512
 HALVES = PIXELS // HALF
-X_TILES = BATCH * HALVES
+QUARTER = HALF // 2
+X_TILES = ((0, 0, HALF), (1, 0, HALF), (2, 0, HALF), (3, 0, QUARTER), (3, QUARTER, QUARTER))
 PSUM_BANKS = 8
 RUN = 4
 
@@ -42,9 +43,12 @@ def tile_self_attention_memory_module_pb_kernel(tc, z, h, m, Wm, bm, out_0, out_
     new_m_tiles = out_1.rearrange("b (q r) i j -> b q r (i j)", r=C_TILES)
     w_tiles = Wm.rearrange("(a q r) k -> a q r k", a=GATES, r=C_TILES)
 
-    def place_of(n):
-        b, half = divmod(n, HALVES)
-        return b, slice(half * HALF, (half + 1) * HALF)
+    def place_of(half, first=0, width=HALF):
+        b, half_of_b = divmod(half, HALVES)
+        return b, slice(half_of_b * HALF + first, half_of_b * HALF + first + width)
+
+    def width_of(n):
+        return X_TILES[n][2]
 
     def pass_rows(b, g):
         if g < Z_PASSES:
@@ -53,7 +57,7 @@ def tile_self_attention_memory_module_pb_kernel(tc, z, h, m, Wm, bm, out_0, out_
 
     with ExitStack() as ctx:
         resident = ctx.enter_context(tc.tile_pool(name="resident", bufs=1))
-        stage = ctx.enter_context(tc.tile_pool(name="stage", bufs=5))
+        stage = ctx.enter_context(tc.tile_pool(name="stage", bufs=8))
         gates = ctx.enter_context(tc.tile_pool(name="gates", bufs=3))
         results = ctx.enter_context(tc.tile_pool(name="results", bufs=8))
         psum = ctx.enter_context(tc.psum_pool(name="psum", bufs=PSUM_BANKS))
@@ -72,7 +76,7 @@ def tile_self_attention_memory_module_pb_kernel(tc, z, h, m, Wm, bm, out_0, out_
         w_raw = [resident.tile([P, GATES, C3], BF16, name="w_raw%d" % r) for r in range(C_TILES)]
         x_raw = [
             [resident.tile([P, PACK, HALF], BF16, name="x_raw%d%d" % (n, g)) for g in range(PASSES)]
-            for n in range(X_TILES)
+            for n in range(BATCH * HALVES)
         ]
         m_sb = [resident.tile([P, C_TILES, PIXELS], BF16, name="m_sb%d" % b) for b in range(BATCH)]
         w_codes = [
@@ -84,12 +88,12 @@ def tile_self_attention_memory_module_pb_kernel(tc, z, h, m, Wm, bm, out_0, out_
             for r in range(C_TILES)
         ]
         x_codes = [
-            resident.tile([P, PASSES * HALF], U32, name="x_codes%d" % n, align_bytes=64)
-            for n in range(X_TILES)
+            resident.tile([P, PASSES * width_of(n)], U32, name="x_codes%d" % n, align_bytes=64)
+            for n in range(len(X_TILES))
         ]
         x_scales = [
-            resident.tile([P, PASSES * HALF], U8, name="x_scales%d" % n, align_bytes=64)
-            for n in range(X_TILES)
+            resident.tile([P, PASSES * width_of(n)], U8, name="x_scales%d" % n, align_bytes=64)
+            for n in range(len(X_TILES))
         ]
 
         def load_w(r, which=GATE_ORDER):
@@ -154,18 +158,19 @@ def tile_self_attention_memory_module_pb_kernel(tc, z, h, m, Wm, bm, out_0, out_
             return [turn_w(r, place, passes) for passes in ((0, 1), (2,))]
 
         def regroup_x(n, g, copy):
+            half, first, width = X_TILES[n]
             grouped = stage.tile([P, HALF, PACK], BF16, name="x_grouped", align_bytes=64)
             copy(
-                out=grouped[:].rearrange("p (c i) t -> p c t i", i=RUN),
-                in_=x_raw[n][g][:].rearrange("p t (c i) -> p c t i", i=RUN),
+                out=grouped[:, :width, :].rearrange("p (c i) t -> p c t i", i=RUN),
+                in_=x_raw[half][g][:, :, first : first + width].rearrange("p t (c i) -> p c t i", i=RUN),
             )
 
             def quantise():
-                cols = slice(g * HALF, (g + 1) * HALF)
+                cols = slice(g * width, (g + 1) * width)
                 nc.vector.quantize_mx(
                     out=x_codes[n][:, cols].bitcast(FP8X4),
                     scales=x_scales[n][:, cols],
-                    in_=grouped[:].rearrange("p w t -> p (w t)"),
+                    in_=grouped[:, :width, :].rearrange("p w t -> p (w t)"),
                 )
 
             return quantise
@@ -185,11 +190,12 @@ def tile_self_attention_memory_module_pb_kernel(tc, z, h, m, Wm, bm, out_0, out_
 
         def multiply(n, r, place):
             acc = psum.tile([P, HALF], F32, tag="bank", name="acc")
+            width = width_of(n)
             for g in range(PASSES):
                 first_w = (place * PASSES + g) * P
-                x_cols = slice(g * HALF, (g + 1) * HALF)
+                x_cols = slice(g * width, (g + 1) * width)
                 nc.tensor.matmul_mx(
-                    out=acc[:],
+                    out=acc[:, :width],
                     lhsT=w_codes[r][:, first_w : first_w + P].bitcast(FP8X4),
                     lhsT_scale=w_scales[r][:, first_w : first_w + P],
                     rhs=x_codes[n][:, x_cols].bitcast(FP8X4),
@@ -197,50 +203,51 @@ def tile_self_attention_memory_module_pb_kernel(tc, z, h, m, Wm, bm, out_0, out_
                     start=(g == 0),
                     stop=(g == PASSES - 1),
                 )
-            return acc
+            return acc[:, :width]
 
         def squash(acc, gate, r, place):
             a = GATE_ORDER[place]
             nc.scalar.activation(
-                out=gate[:],
-                in_=acc[:],
+                out=gate,
+                in_=acc,
                 func=ACT.Tanh if a == CANDIDATE else ACT.Sigmoid,
                 bias=bias[:, a, r : r + 1],
                 scale=1.0,
             )
 
         def new_unit(n, r):
+            width = width_of(n)
             return {
                 "n": n,
                 "r": r,
-                "cand": results.tile([P, HALF], F32, name="cand"),
-                "gate_i": gates.tile([P, HALF], F32, name="gate_i"),
-                "gate_o": results.tile([P, HALF], F32, name="gate_o"),
+                "cand": results.tile([P, HALF], F32, name="cand")[:, :width],
+                "gate_i": gates.tile([P, HALF], F32, name="gate_i")[:, :width],
+                "gate_o": results.tile([P, HALF], F32, name="gate_o")[:, :width],
             }
 
         def memory(unit):
-            b, cols = place_of(unit["n"])
+            b, cols = place_of(*X_TILES[unit["n"]])
             return m_sb[b][:, unit["r"], cols]
 
         def store(out_tiles, unit, name):
-            b, cols = place_of(unit["n"])
-            nc.sync.dma_start(out=out_tiles[b][:, unit["r"], cols], in_=unit[name][:])
+            b, cols = place_of(*X_TILES[unit["n"]])
+            nc.sync.dma_start(out=out_tiles[b][:, unit["r"], cols], in_=unit[name])
 
         def no_step(unit):
             pass
 
         def difference(unit):
-            nc.vector.tensor_sub(out=unit["cand"][:], in0=unit["cand"][:], in1=memory(unit))
+            nc.vector.tensor_sub(out=unit["cand"], in0=unit["cand"], in1=memory(unit))
 
         def gated_step(unit):
-            nc.vector.tensor_mul(out=unit["cand"][:], in0=unit["gate_i"][:], in1=unit["cand"][:])
+            nc.vector.tensor_mul(out=unit["cand"], in0=unit["gate_i"], in1=unit["cand"])
 
         def new_memory(unit):
-            nc.vector.tensor_add(out=unit["cand"][:], in0=unit["cand"][:], in1=memory(unit))
+            nc.vector.tensor_add(out=unit["cand"], in0=unit["cand"], in1=memory(unit))
             store(new_m_tiles, unit, "cand")
 
         def new_hidden(unit):
-            nc.vector.tensor_mul(out=unit["gate_o"][:], in0=unit["gate_o"][:], in1=unit["cand"][:])
+            nc.vector.tensor_mul(out=unit["gate_o"], in0=unit["gate_o"], in1=unit["cand"])
             store(new_h_tiles, unit, "gate_o")
 
         first_gate = turn_gate(0, 0)
@@ -262,22 +269,28 @@ def tile_self_attention_memory_module_pb_kernel(tc, z, h, m, Wm, bm, out_0, out_
             (1, 0, None, [(2, 0, 0, on_vector), (2, 1, 1, on_vector), (2, 2, 2, on_scalar)]),
             (1, 1, None, []),
             (0, 2, 3, []),
-            (1, 2, None, [(3, 0, 0, on_vector)]),
+            (1, 2, None, [(3, 0, 0, on_scalar)]),
             (2, 0, None, [(3, 1, 0, on_scalar)]),
             (2, 1, None, [(3, 2, 0, on_scalar)]),
-            (2, 2, None, []),
-            (0, 3, None, []),
-            (1, 3, None, []),
+            (2, 2, None, [(4, 0, 0, on_scalar)]),
+            (0, 3, None, [(4, 1, 0, on_scalar)]),
+            (1, 3, None, [(4, 2, 0, on_scalar)]),
             (2, 3, None, []),
             (3, 0, None, []),
             (3, 1, None, []),
             (3, 2, None, []),
             (3, 3, None, []),
+            (4, 0, None, []),
+            (4, 1, None, []),
+            (4, 2, None, []),
+            (4, 3, None, []),
         ]
         earlier = None
+        copied_by_scalar = []
         for n, r, next_tile, x_passes in plan:
             unit = new_unit(n, r)
-            extras = []
+            extras = copied_by_scalar
+            copied_by_scalar = []
             for place, name in enumerate(("cand", "gate_i", "gate_o")):
                 squash(multiply(n, r, place), unit[name], r, place)
                 if earlier is None and place == 0:
@@ -289,7 +302,10 @@ def tile_self_attention_memory_module_pb_kernel(tc, z, h, m, Wm, bm, out_0, out_
                     extras += turn_gate(next_tile, place)
                 for x_tile, g, behind, copy in x_passes:
                     if behind == place:
-                        extras += [regroup_x(x_tile, g, copy)] if copy is on_scalar else regroup_later(x_tile, g)
+                        if copy is on_scalar:
+                            copied_by_scalar.append(regroup_x(x_tile, g, copy))
+                        else:
+                            extras += regroup_later(x_tile, g)
             steps = [(difference, unit), (new_memory, earlier), (gated_step, unit), (new_hidden, earlier)]
             if earlier is None:
                 steps = [(no_step, unit), (no_step, unit), (gated_step, unit), (no_step, unit)]

@@ -28,6 +28,9 @@ HALVES = PIXELS // HALF
 QUARTER = HALF // 2
 X_TILES = ((0, 0, HALF), (1, 0, HALF), (2, 0, HALF), (3, 0, QUARTER), (3, QUARTER, QUARTER))
 PSUM_BANKS = 8
+CHUNKS_PER_BANK = 2
+W_GROUP = 4
+TURNED_BEHIND = (((0, 4), (4, 2)), ((6, 2), (8, 1)), ())
 RUN = 4
 
 FLOPS = 2 * C3 * C3 * BATCH * PIXELS
@@ -57,7 +60,8 @@ def tile_self_attention_memory_module_pb_kernel(tc, z, h, m, Wm, bm, out_0, out_
 
     with ExitStack() as ctx:
         resident = ctx.enter_context(tc.tile_pool(name="resident", bufs=1))
-        stage = ctx.enter_context(tc.tile_pool(name="stage", bufs=8))
+        w_stage = ctx.enter_context(tc.tile_pool(name="w_stage", bufs=5))
+        x_stage = ctx.enter_context(tc.tile_pool(name="x_stage", bufs=6))
         gates = ctx.enter_context(tc.tile_pool(name="gates", bufs=3))
         results = ctx.enter_context(tc.tile_pool(name="results", bufs=8))
         psum = ctx.enter_context(tc.psum_pool(name="psum", bufs=PSUM_BANKS))
@@ -130,36 +134,40 @@ def tile_self_attention_memory_module_pb_kernel(tc, z, h, m, Wm, bm, out_0, out_
         load_x(3)
         load_m(1, 3)
 
-        def turn_w(r, place, passes):
-            count = len(passes)
-            turned = psum.tile([P, 2, 2, P], F32, tag="bank")
-            words = w_raw[r][:, GATE_ORDER[place], :].bitcast(F32)
-            for s, g in enumerate(passes):
-                for u in range(2):
-                    every_second = slice(g * 2 * P + u, (g + 1) * 2 * P, 2)
-                    nc.tensor.transpose(turned[:, s, u, :], words[:, every_second], ident[:])
-            grouped = stage.tile([P, 2 * P * PACK], BF16, name="w_grouped", align_bytes=64)
-            columns = grouped[:, : count * P * PACK]
-            nc.scalar.copy(
-                out=columns.bitcast(F32).rearrange("p (s o u) -> p s o u", s=count, u=2),
-                in_=turned[:, :count, :, :].rearrange("p s u o -> p s o u"),
-            )
+        def turn_w(r, first, count):
+            width = P * PACK
+            grouped = w_stage.tile([P, W_GROUP * width], BF16, name="w_grouped", align_bytes=64)
+            for done in range(0, count, CHUNKS_PER_BANK):
+                chunks = range(done, min(done + CHUNKS_PER_BANK, count))
+                turned = psum.tile([P, CHUNKS_PER_BANK, 2, P], F32, tag="bank")
+                for s, chunk in enumerate(chunks):
+                    place, g = divmod(first + chunk, PASSES)
+                    words = w_raw[r][:, GATE_ORDER[place], :].bitcast(F32)
+                    for u in range(2):
+                        every_second = slice(g * 2 * P + u, (g + 1) * 2 * P, 2)
+                        nc.tensor.transpose(turned[:, s, u, :], words[:, every_second], ident[:])
+                columns = grouped[:, chunks.start * width : chunks.stop * width]
+                nc.scalar.copy(
+                    out=columns.bitcast(F32).rearrange("p (s o u) -> p s o u", s=len(chunks), u=2),
+                    in_=turned[:, : len(chunks), :, :].rearrange("p s u o -> p s o u"),
+                )
 
             def quantise():
-                first = (place * PASSES + passes[0]) * P
-                cols = slice(first, first + count * P)
+                cols = slice(first * P, (first + count) * P)
                 nc.vector.quantize_mx(
-                    out=w_codes[r][:, cols].bitcast(FP8X4), scales=w_scales[r][:, cols], in_=columns
+                    out=w_codes[r][:, cols].bitcast(FP8X4),
+                    scales=w_scales[r][:, cols],
+                    in_=grouped[:, : count * width],
                 )
 
             return quantise
 
         def turn_gate(r, place):
-            return [turn_w(r, place, passes) for passes in ((0, 1), (2,))]
+            return [turn_w(r, place * PASSES + first, count) for first, count in ((0, 2), (2, 1))]
 
         def regroup_x(n, g, copy):
             half, first, width = X_TILES[n]
-            grouped = stage.tile([P, HALF, PACK], BF16, name="x_grouped", align_bytes=64)
+            grouped = x_stage.tile([P, HALF, PACK], BF16, name="x_grouped", align_bytes=64)
             copy(
                 out=grouped[:, :width, :].rearrange("p (c i) t -> p c t i", i=RUN),
                 in_=x_raw[half][g][:, :, first : first + width].rearrange("p t (c i) -> p c t i", i=RUN),
@@ -215,35 +223,46 @@ def tile_self_attention_memory_module_pb_kernel(tc, z, h, m, Wm, bm, out_0, out_
                 scale=1.0,
             )
 
-        def new_unit(n, r):
-            width = width_of(n)
+        def new_unit(n, tiles):
+            size = len(tiles) * width_of(n)
             return {
                 "n": n,
-                "r": r,
-                "cand": results.tile([P, HALF], F32, name="cand")[:, :width],
-                "gate_i": gates.tile([P, HALF], F32, name="gate_i")[:, :width],
-                "gate_o": results.tile([P, HALF], F32, name="gate_o")[:, :width],
+                "tiles": tiles,
+                "cand": results.tile([P, HALF], F32, name="cand")[:, :size],
+                "gate_i": gates.tile([P, HALF], F32, name="gate_i")[:, :size],
+                "gate_o": results.tile([P, HALF], F32, name="gate_o")[:, :size],
             }
 
-        def memory(unit):
+        def part(unit, name, i):
+            width = width_of(unit["n"])
+            return unit[name][:, i * width : (i + 1) * width]
+
+        def by_tile(unit, name):
+            return unit[name].rearrange("p (r w) -> p r w", r=len(unit["tiles"]))
+
+        def rows_of(unit, of_batch):
             b, cols = place_of(*X_TILES[unit["n"]])
-            return m_sb[b][:, unit["r"], cols]
+            return of_batch[b][:, unit["tiles"][0] : unit["tiles"][-1] + 1, cols]
+
+        def memory(unit):
+            return rows_of(unit, m_sb)
 
         def store(out_tiles, unit, name):
-            b, cols = place_of(*X_TILES[unit["n"]])
-            nc.sync.dma_start(out=out_tiles[b][:, unit["r"], cols], in_=unit[name])
+            nc.sync.dma_start(out=rows_of(unit, out_tiles), in_=by_tile(unit, name))
 
         def no_step(unit):
             pass
 
         def difference(unit):
-            nc.vector.tensor_sub(out=unit["cand"], in0=unit["cand"], in1=memory(unit))
+            cand = by_tile(unit, "cand")
+            nc.vector.tensor_sub(out=cand, in0=cand, in1=memory(unit))
 
         def gated_step(unit):
             nc.vector.tensor_mul(out=unit["cand"], in0=unit["gate_i"], in1=unit["cand"])
 
         def new_memory(unit):
-            nc.vector.tensor_add(out=unit["cand"], in0=unit["cand"], in1=memory(unit))
+            cand = by_tile(unit, "cand")
+            nc.vector.tensor_add(out=cand, in0=cand, in1=memory(unit))
             store(new_m_tiles, unit, "cand")
 
         def new_hidden(unit):
@@ -264,52 +283,55 @@ def tile_self_attention_memory_module_pb_kernel(tc, z, h, m, Wm, bm, out_0, out_
             quantise()
 
         plan = [
-            (0, 0, 1, [(1, 0, 0, on_vector), (1, 1, 1, on_vector), (1, 2, 2, on_scalar)]),
-            (0, 1, 2, []),
-            (1, 0, None, [(2, 0, 0, on_vector), (2, 1, 1, on_vector), (2, 2, 2, on_scalar)]),
-            (1, 1, None, []),
-            (0, 2, 3, []),
-            (1, 2, None, [(3, 0, 0, on_scalar)]),
-            (2, 0, None, [(3, 1, 0, on_scalar)]),
-            (2, 1, None, [(3, 2, 0, on_scalar)]),
-            (2, 2, None, [(4, 0, 0, on_scalar)]),
-            (0, 3, None, [(4, 1, 0, on_scalar)]),
-            (1, 3, None, [(4, 2, 0, on_scalar)]),
-            (2, 3, None, []),
-            (3, 0, None, []),
-            (3, 1, None, []),
-            (3, 2, None, []),
-            (3, 3, None, []),
-            (4, 0, None, []),
-            (4, 1, None, []),
-            (4, 2, None, []),
-            (4, 3, None, []),
+            (0, (0,), 1, [(1, 0, 0, on_vector), (1, 1, 1, on_vector), (1, 2, 2, on_scalar)]),
+            (0, (1,), 2, [(2, 0, 1, on_vector)]),
+            (1, (0,), None, [(2, 1, 1, on_vector), (2, 2, 1, on_scalar)]),
+            (1, (1,), None, []),
+            (0, (2,), None, []),
+            (1, (2,), 3, [(3, 0, 1, on_scalar)]),
+            (2, (0,), None, [(3, 1, 1, on_scalar)]),
+            (2, (1,), None, [(3, 2, 1, on_scalar)]),
+            (2, (2,), None, []),
+            (0, (3,), None, []),
+            (1, (3,), None, [(4, 0, 1, on_scalar)]),
+            (2, (3,), None, [(4, 1, 1, on_scalar)]),
+            (3, (0, 1), None, [(4, 2, 1, on_scalar)]),
+            (3, (2, 3), None, []),
+            (4, (0, 1), None, []),
+            (4, (2,), None, []),
+            (4, (3,), None, []),
         ]
         earlier = None
         copied_by_scalar = []
-        for n, r, next_tile, x_passes in plan:
-            unit = new_unit(n, r)
+        for n, tiles, next_tile, x_passes in plan:
+            unit = new_unit(n, tiles)
             extras = copied_by_scalar
             copied_by_scalar = []
             for place, name in enumerate(("cand", "gate_i", "gate_o")):
-                squash(multiply(n, r, place), unit[name], r, place)
+                for i, r in enumerate(tiles):
+                    squash(multiply(n, r, place), part(unit, name, i), r, place)
                 if earlier is None and place == 0:
                     third_gate = turn_gate(0, 2)
                     difference(unit)
                     for quantise in third_gate:
                         quantise()
+                here = [(x_tile, g, copy) for x_tile, g, behind, copy in x_passes if behind == place]
+                on_vector_here = [regroup_later(x_tile, g) for x_tile, g, copy in here if copy is on_vector]
+                extras += [regroup for regroup, quantise in on_vector_here]
                 if next_tile is not None:
-                    extras += turn_gate(next_tile, place)
-                for x_tile, g, behind, copy in x_passes:
-                    if behind == place:
-                        if copy is on_scalar:
-                            copied_by_scalar.append(regroup_x(x_tile, g, copy))
-                        else:
-                            extras += regroup_later(x_tile, g)
+                    extras += [turn_w(next_tile, *chunks) for chunks in TURNED_BEHIND[place]]
+                extras += [quantise for regroup, quantise in on_vector_here]
+                for x_tile, g, copy in here:
+                    if copy is on_scalar:
+                        copied_by_scalar.append(regroup_x(x_tile, g, copy))
             steps = [(difference, unit), (new_memory, earlier), (gated_step, unit), (new_hidden, earlier)]
             if earlier is None:
                 steps = [(no_step, unit), (no_step, unit), (gated_step, unit), (no_step, unit)]
-            bounds = [(len(extras) * j + len(steps) - 1) // len(steps) for j in range(len(steps) + 1)]
+            bounds = [min(1, len(extras))]
+            for j in range(len(steps)):
+                bounds.append(max(bounds[-1], (len(extras) * (j + 1) + len(steps) - 1) // len(steps)))
+            for extra in extras[: bounds[0]]:
+                extra()
             for j, (step, of_unit) in enumerate(steps):
                 step(of_unit)
                 for extra in extras[bounds[j] : bounds[j + 1]]:

from contextlib import ExitStack

import concourse.mybir as mybir
from concourse.masks import make_identity

F32 = mybir.dt.float32
BF16 = mybir.dt.bfloat16
U32 = mybir.dt.uint32
U8 = mybir.dt.uint8
FP8X4 = mybir.dt.float8_e4m3fn_x4
ACT = mybir.ActivationFunctionType

P = 128
PACK = 4
K_PASS = P * PACK
BATCH = 2
C = 512
C3 = 3 * C
PIXELS = 1024
PASSES = C3 // K_PASS
Z_PASSES = 2
GATES = 3
OUT_GATE, CANDIDATE, IN_GATE = 0, 1, 2
GATE_ORDER = (CANDIDATE, IN_GATE, OUT_GATE)
C_TILES = C // P
HALF = 512
HALVES = PIXELS // HALF
QUARTER = HALF // 2
X_TILES = ((0, 0, HALF), (1, 0, HALF), (2, 0, HALF), (3, 0, QUARTER), (3, QUARTER, QUARTER))
PSUM_BANKS = 8
CHUNKS_PER_BANK = 2
W_GROUP = 4
TURNED_BEHIND = (((0, 4), (4, 2)), ((6, 2), (8, 1)), ())
RUN = 4

FLOPS = 2 * C3 * C3 * BATCH * PIXELS


def tile_self_attention_memory_module_pb_kernel(tc, z, h, m, Wm, bm, out_0, out_1):
    nc = tc.nc

    z_rows = z.rearrange("b c i j -> b c (i j)")
    h_rows = h.rearrange("b c i j -> b c (i j)")
    m_tiles = m.rearrange("b (q r) i j -> b q r (i j)", r=C_TILES)
    new_h_tiles = out_0.rearrange("b (q r) i j -> b q r (i j)", r=C_TILES)
    new_m_tiles = out_1.rearrange("b (q r) i j -> b q r (i j)", r=C_TILES)
    w_tiles = Wm.rearrange("(a q r) k -> a q r k", a=GATES, r=C_TILES)

    def place_of(half, first=0, width=HALF):
        b, half_of_b = divmod(half, HALVES)
        return b, slice(half_of_b * HALF + first, half_of_b * HALF + first + width)

    def width_of(n):
        return X_TILES[n][2]

    def pass_rows(b, g):
        if g < Z_PASSES:
            return z_rows[b, g * K_PASS : (g + 1) * K_PASS, :]
        return h_rows[b]

    with ExitStack() as ctx:
        resident = ctx.enter_context(tc.tile_pool(name="resident", bufs=1))
        w_stage = ctx.enter_context(tc.tile_pool(name="w_stage", bufs=5))
        x_stage = ctx.enter_context(tc.tile_pool(name="x_stage", bufs=6))
        gates = ctx.enter_context(tc.tile_pool(name="gates", bufs=3))
        results = ctx.enter_context(tc.tile_pool(name="results", bufs=8))
        psum = ctx.enter_context(tc.psum_pool(name="psum", bufs=PSUM_BANKS))

        warm = resident.tile([P, 1], F32)
        nc.vector.memset(warm[:], 0.0)
        warm_out = resident.tile([P, 1], F32)
        nc.scalar.activation(out=warm_out[:], in_=warm[:], func=ACT.Sigmoid)

        ident = resident.tile([P, P], F32)
        make_identity(nc, ident[:])

        ctx.enter_context(tc.manual_schedule())

        bias = resident.tile([P, GATES, C_TILES], BF16)
        w_raw = [resident.tile([P, GATES, C3], BF16, name="w_raw%d" % r) for r in range(C_TILES)]
        x_raw = [
            [resident.tile([P, PACK, HALF], BF16, name="x_raw%d%d" % (n, g)) for g in range(PASSES)]
            for n in range(BATCH * HALVES)
        ]
        m_sb = [resident.tile([P, C_TILES, PIXELS], BF16, name="m_sb%d" % b) for b in range(BATCH)]
        w_codes = [
            resident.tile([P, GATES * PASSES * P], U32, name="w_codes%d" % r, align_bytes=64)
            for r in range(C_TILES)
        ]
        w_scales = [
            resident.tile([P, GATES * PASSES * P], U8, name="w_scales%d" % r, align_bytes=64)
            for r in range(C_TILES)
        ]
        x_codes = [
            resident.tile([P, PASSES * width_of(n)], U32, name="x_codes%d" % n, align_bytes=64)
            for n in range(len(X_TILES))
        ]
        x_scales = [
            resident.tile([P, PASSES * width_of(n)], U8, name="x_scales%d" % n, align_bytes=64)
            for n in range(len(X_TILES))
        ]

        def load_w(r, which=GATE_ORDER):
            for a in which:
                nc.sync.dma_start(out=w_raw[r][:, a, :], in_=w_tiles[a][:, r, :])

        def load_x(n):
            b, cols = place_of(n)
            for g in range(PASSES):
                nc.sync.dma_start(
                    out=x_raw[n][g][:],
                    in_=pass_rows(b, g)[:, cols].rearrange("(p t) w -> p t w", t=PACK),
                )

        def load_m(b, r):
            nc.sync.dma_start(out=m_sb[b][:, r, :], in_=m_tiles[b][:, r, :])

        load_w(0, GATE_ORDER[:1])
        load_x(0)
        load_w(0, GATE_ORDER[1:])
        nc.sync.dma_start(out=bias[:], in_=bm.rearrange("(a q r) -> q a r", a=GATES, r=C_TILES))
        load_m(0, 0)
        load_w(1)
        load_m(0, 1)
        load_x(1)
        load_w(2)
        load_m(0, 2)
        load_x(2)
        load_m(1, 0)
        load_m(1, 1)
        load_w(3)
        load_m(1, 2)
        load_m(0, 3)
        load_x(3)
        load_m(1, 3)

        def turn_w(r, first, count):
            width = P * PACK
            grouped = w_stage.tile([P, W_GROUP * width], BF16, name="w_grouped", align_bytes=64)
            for done in range(0, count, CHUNKS_PER_BANK):
                chunks = range(done, min(done + CHUNKS_PER_BANK, count))
                turned = psum.tile([P, CHUNKS_PER_BANK, 2, P], F32, tag="bank")
                for s, chunk in enumerate(chunks):
                    place, g = divmod(first + chunk, PASSES)
                    words = w_raw[r][:, GATE_ORDER[place], :].bitcast(F32)
                    for u in range(2):
                        every_second = slice(g * 2 * P + u, (g + 1) * 2 * P, 2)
                        nc.tensor.transpose(turned[:, s, u, :], words[:, every_second], ident[:])
                columns = grouped[:, chunks.start * width : chunks.stop * width]
                nc.scalar.copy(
                    out=columns.bitcast(F32).rearrange("p (s o u) -> p s o u", s=len(chunks), u=2),
                    in_=turned[:, : len(chunks), :, :].rearrange("p s u o -> p s o u"),
                )

            def quantise():
                cols = slice(first * P, (first + count) * P)
                nc.vector.quantize_mx(
                    out=w_codes[r][:, cols].bitcast(FP8X4),
                    scales=w_scales[r][:, cols],
                    in_=grouped[:, : count * width],
                )

            return quantise

        def turn_gate(r, place):
            return [turn_w(r, place * PASSES + first, count) for first, count in ((0, 2), (2, 1))]

        def regroup_x(n, g, copy):
            half, first, width = X_TILES[n]
            grouped = x_stage.tile([P, HALF, PACK], BF16, name="x_grouped", align_bytes=64)
            copy(
                out=grouped[:, :width, :].rearrange("p (c i) t -> p c t i", i=RUN),
                in_=x_raw[half][g][:, :, first : first + width].rearrange("p t (c i) -> p c t i", i=RUN),
            )

            def quantise():
                cols = slice(g * width, (g + 1) * width)
                nc.vector.quantize_mx(
                    out=x_codes[n][:, cols].bitcast(FP8X4),
                    scales=x_scales[n][:, cols],
                    in_=grouped[:, :width, :].rearrange("p w t -> p (w t)"),
                )

            return quantise

        on_vector, on_scalar = nc.vector.tensor_copy, nc.scalar.copy

        def regroup_later(n, g):
            made = []

            def regroup():
                made.append(regroup_x(n, g, on_vector))

            def quantise():
                made[0]()

            return [regroup, quantise]

        def multiply(n, r, place):
            acc = psum.tile([P, HALF], F32, tag="bank", name="acc")
            width = width_of(n)
            for g in range(PASSES):
                first_w = (place * PASSES + g) * P
                x_cols = slice(g * width, (g + 1) * width)
                nc.tensor.matmul_mx(
                    out=acc[:, :width],
                    lhsT=w_codes[r][:, first_w : first_w + P].bitcast(FP8X4),
                    lhsT_scale=w_scales[r][:, first_w : first_w + P],
                    rhs=x_codes[n][:, x_cols].bitcast(FP8X4),
                    rhs_scale=x_scales[n][:, x_cols],
                    start=(g == 0),
                    stop=(g == PASSES - 1),
                )
            return acc[:, :width]

        def squash(acc, gate, r, place):
            a = GATE_ORDER[place]
            nc.scalar.activation(
                out=gate,
                in_=acc,
                func=ACT.Tanh if a == CANDIDATE else ACT.Sigmoid,
                bias=bias[:, a, r : r + 1],
                scale=1.0,
            )

        def new_unit(n, tiles):
            size = len(tiles) * width_of(n)
            return {
                "n": n,
                "tiles": tiles,
                "cand": results.tile([P, HALF], F32, name="cand")[:, :size],
                "gate_i": gates.tile([P, HALF], F32, name="gate_i")[:, :size],
                "gate_o": results.tile([P, HALF], F32, name="gate_o")[:, :size],
            }

        def part(unit, name, i):
            width = width_of(unit["n"])
            return unit[name][:, i * width : (i + 1) * width]

        def by_tile(unit, name):
            return unit[name].rearrange("p (r w) -> p r w", r=len(unit["tiles"]))

        def rows_of(unit, of_batch):
            b, cols = place_of(*X_TILES[unit["n"]])
            return of_batch[b][:, unit["tiles"][0] : unit["tiles"][-1] + 1, cols]

        def memory(unit):
            return rows_of(unit, m_sb)

        def store(out_tiles, unit, name):
            nc.sync.dma_start(out=rows_of(unit, out_tiles), in_=by_tile(unit, name))

        def no_step(unit):
            pass

        def difference(unit):
            cand = by_tile(unit, "cand")
            nc.vector.tensor_sub(out=cand, in0=cand, in1=memory(unit))

        def gated_step(unit):
            nc.vector.tensor_mul(out=unit["cand"], in0=unit["gate_i"], in1=unit["cand"])

        def new_memory(unit):
            cand = by_tile(unit, "cand")
            nc.vector.tensor_add(out=cand, in0=cand, in1=memory(unit))
            store(new_m_tiles, unit, "cand")

        def new_hidden(unit):
            nc.vector.tensor_mul(out=unit["gate_o"], in0=unit["gate_o"], in1=unit["cand"])
            store(new_h_tiles, unit, "gate_o")

        first_gate = turn_gate(0, 0)
        x_first = regroup_x(0, 0, on_vector)
        x_second = regroup_x(0, 1, on_scalar)
        first_gate[0]()
        x_first()
        first_gate[1]()
        x_third = regroup_x(0, 2, on_vector)
        x_second()
        second_gate = turn_gate(0, 1)
        x_third()
        for quantise in second_gate:
            quantise()

        plan = [
            (0, (0,), 1, [(1, 0, 0, on_vector), (1, 1, 1, on_vector), (1, 2, 2, on_scalar)]),
            (0, (1,), 2, [(2, 0, 1, on_vector)]),
            (1, (0,), None, [(2, 1, 1, on_vector), (2, 2, 1, on_scalar)]),
            (1, (1,), None, []),
            (0, (2,), None, []),
            (1, (2,), 3, [(3, 0, 1, on_scalar)]),
            (2, (0,), None, [(3, 1, 1, on_scalar)]),
            (2, (1,), None, [(3, 2, 1, on_scalar)]),
            (2, (2,), None, []),
            (0, (3,), None, []),
            (1, (3,), None, [(4, 0, 1, on_scalar)]),
            (2, (3,), None, [(4, 1, 1, on_scalar)]),
            (3, (0, 1), None, [(4, 2, 1, on_scalar)]),
            (3, (2, 3), None, []),
            (4, (0, 1), None, []),
            (4, (2,), None, []),
            (4, (3,), None, []),
        ]
        earlier = None
        copied_by_scalar = []
        for n, tiles, next_tile, x_passes in plan:
            unit = new_unit(n, tiles)
            extras = copied_by_scalar
            copied_by_scalar = []
            for place, name in enumerate(("cand", "gate_i", "gate_o")):
                for i, r in enumerate(tiles):
                    squash(multiply(n, r, place), part(unit, name, i), r, place)
                if earlier is None and place == 0:
                    third_gate = turn_gate(0, 2)
                    difference(unit)
                    for quantise in third_gate:
                        quantise()
                here = [(x_tile, g, copy) for x_tile, g, behind, copy in x_passes if behind == place]
                on_vector_here = [regroup_later(x_tile, g) for x_tile, g, copy in here if copy is on_vector]
                extras += [regroup for regroup, quantise in on_vector_here]
                if next_tile is not None:
                    extras += [turn_w(next_tile, *chunks) for chunks in TURNED_BEHIND[place]]
                extras += [quantise for regroup, quantise in on_vector_here]
                for x_tile, g, copy in here:
                    if copy is on_scalar:
                        copied_by_scalar.append(regroup_x(x_tile, g, copy))
            steps = [(difference, unit), (new_memory, earlier), (gated_step, unit), (new_hidden, earlier)]
            if earlier is None:
                steps = [(no_step, unit), (no_step, unit), (gated_step, unit), (no_step, unit)]
            bounds = [min(1, len(extras))]
            for j in range(len(steps)):
                bounds.append(max(bounds[-1], (len(extras) * (j + 1) + len(steps) - 1) // len(steps)))
            for extra in extras[: bounds[0]]:
                extra()
            for j, (step, of_unit) in enumerate(steps):
                step(of_unit)
                for extra in extras[bounds[j] : bounds[j + 1]]:
                    extra()
            earlier = unit
        new_memory(earlier)
        new_hidden(earlier)
